import numpy as np
import ml_dtypes


def mxq(x, axis, fmt="e4m3"):
    dtype, down = {"e4m3": (ml_dtypes.float8_e4m3fn, 7), "e5m2": (ml_dtypes.float8_e5m2, 14)}[fmt]
    v = np.moveaxis(np.asarray(x, np.float32).astype(ml_dtypes.bfloat16).astype(np.float64), axis, -1)
    blocks = v.reshape(v.shape[:-1] + (-1, 32))
    amax = np.abs(blocks).max(-1, keepdims=True)
    byte = np.maximum(np.where(amax > 0, np.frexp(amax)[1] - 1 + 127, 0) - down, 1)
    scale = np.exp2(byte - 127.0)
    codes = (blocks / scale).astype(np.float32).astype(dtype).astype(np.float64)
    return np.moveaxis((codes * scale).reshape(v.shape), -1, axis)


WIDE = False


def mx_kscale(k):
    if not WIDE:
        return np.ones(k)
    levels = np.array([10, -10, 5, -5, 0])
    a = np.random.permutation(np.resize(levels, k // 512 * 4)).reshape(k // 512, 4)
    idx = np.arange(k)
    return np.exp2(a[idx // 512, idx % 128 // 32])


BF16 = ml_dtypes.bfloat16


def bf(x):
    return np.asarray(x, np.float32).astype(BF16)


def f64(x):
    return np.asarray(x).astype(np.float64)


B, T, H, N = 4, 256, 1024, 1024


def setup_inputs():
    s = mx_kscale(H)
    t = np.exp2(np.round(np.log2(s) / 2))
    d = float(s.min())
    even = (np.arange(N) % 2 == 0)[:, None]
    f = np.where(even, t[None, :] * d ** 6, 1.0 / t[None, :])
    return {"h_time": bf(np.random.standard_normal((B, T, H)) * t * d ** 6),
            "E_dyn": bf(np.random.standard_normal((N, H)) * 0.25 * f)}


def reference(h_time, E_dyn):
    h_mean = f64(h_time).mean(axis=(0, 1))
    E = f64(E_dyn) + h_mean[None, :]
    E_cur = E / np.maximum(np.sqrt((E * E).sum(-1, keepdims=True)), 1e-12)
    Eq = mxq(E_cur, 1, "e4m3")
    G = np.maximum(Eq @ Eq.T, 0.0)
    P = G / (G.sum(-1, keepdims=True) + 1e-6)
    return 0.5 * (P + P.T)

@@ -1,0 +1,221 @@
+from contextlib import ExitStack
+
+import concourse.mybir as mybir
+from concourse.masks import make_identity
+
+F32 = mybir.dt.float32
+BF16 = mybir.dt.bfloat16
+U32 = mybir.dt.uint32
+U8 = mybir.dt.uint8
+FP8X4 = mybir.dt.float8_e4m3fn_x4
+ALU = mybir.AluOpType
+ACT = mybir.ActivationFunctionType
+AXIS = mybir.AxisListType
+
+P = 128
+NODES = 1024
+FEATS = 1024
+H_ROWS = 1024
+TILES = NODES // P
+SLICES = H_ROWS // P
+BLOCKS = FEATS // P
+PACK = 4
+PASSES = FEATS // (P * PACK)
+BANK = 512
+HALVES = NODES // BANK
+ONES = 8
+
+NORM_FLOOR = 1e-12
+ROWSUM_EPS = 1e-6
+SQRT_GUARD = 2.0 ** -110
+
+FLOPS = 2 * NODES * NODES * FEATS
+
+
+def tile_gateddynamicfusion_pa_kernel(tc, h_time, E_dyn, out):
+    nc = tc.nc
+    h_rows = h_time.flatten_outer_dims().rearrange("(p s) k -> p s k", s=SLICES)
+    e_rows = E_dyn.rearrange("(t p) k -> p t k", p=P)
+    out_rows = out.rearrange("(t p) j -> p t j", p=P)
+
+    with ExitStack() as ctx:
+        keep = ctx.enter_context(tc.tile_pool(name="keep", bufs=1))
+        work = ctx.enter_context(tc.tile_pool(name="work", bufs=3))
+
+        h_sb = keep.tile([P, SLICES, FEATS], BF16)
+        e_sb = keep.tile([P, TILES, FEATS], BF16)
+        for s in range(0, SLICES, 2):
+            nc.sync.dma_start(out=h_sb[:, s : s + 2, :], in_=h_rows[:, s : s + 2, :])
+        for t in range(0, TILES, 2):
+            nc.sync.dma_start(out=e_sb[:, t : t + 2, :], in_=e_rows[:, t : t + 2, :])
+
+        ident_f32 = keep.tile([P, P], F32)
+        make_identity(nc, ident_f32[:])
+        ident_bf16 = keep.tile([P, P], BF16)
+        make_identity(nc, ident_bf16[:])
+        ones = keep.tile([P, ONES], BF16)
+        nc.vector.memset(ones[:], 1.0)
+        one = keep.tile([P, 1], F32)
+        nc.vector.memset(one[:], 1.0)
+        warm = keep.tile([P, 1], F32)
+        nc.scalar.activation(out=warm[:], in_=one[:], func=ACT.Sqrt)
+
+        codes = keep.tile([P, PASSES, NODES], U32, align_bytes=64)
+        scales = keep.tile([P, PASSES, NODES], U8, align_bytes=64)
+        g_sb = keep.tile([P, TILES, NODES], F32)
+        w_free = keep.tile([P, NODES], F32)
+
+        sumsq = keep.tile([P, TILES], F32)
+        norm = keep.tile([P, TILES], F32)
+        floored = keep.tile([P, TILES], F32)
+        inv_norm = keep.tile([P, TILES], F32)
+        half_sums = keep.tile([P, TILES, HALVES], F32)
+        row_sum = keep.tile([P, TILES], F32)
+        denom = keep.tile([P, TILES], F32)
+        w_part = keep.tile([P, TILES], F32)
+
+        with tc.psum_pool(name="front_psum", bufs=1) as front_psum:
+            h_part = front_psum.tile([P, BLOCKS, SLICES, ONES], F32)
+            for s in range(SLICES):
+                for j in range(BLOCKS):
+                    nc.tensor.matmul(
+                        out=h_part[:, j, s, :],
+                        lhsT=h_sb[:, s, j * P : (j + 1) * P],
+                        rhs=ones[:],
+                        start=True,
+                        stop=True,
+                    )
+            h_sum = keep.tile([P, BLOCKS], F32)
+            nc.vector.tensor_reduce(out=h_sum[:], in_=h_part[:, :, :, 0], axis=AXIS.X, op=ALU.add)
+            h_rep = keep.tile([P, BLOCKS, P], F32)
+            half = BLOCKS // 2
+            nc.vector.tensor_scalar(
+                out=h_rep[:, 0:half, :],
+                in0=h_sum[:, 0:half].unsqueeze(2).to_broadcast([P, half, P]),
+                scalar1=1.0 / H_ROWS,
+                scalar2=None,
+                op0=ALU.mult,
+            )
+            nc.scalar.activation(
+                out=h_rep[:, half:BLOCKS, :],
+                in_=h_sum[:, half:BLOCKS].unsqueeze(2).to_broadcast([P, half, P]),
+                func=ACT.Copy,
+                scale=1.0 / H_ROWS,
+            )
+            h_mean = [
+                front_psum.tile([P, BANK], F32, name="h_mean%d" % b) for b in range(FEATS // BANK)
+            ]
+            for j in range(BLOCKS):
+                b, c = divmod(j * P, BANK)
+                nc.tensor.transpose(h_mean[b][:, c : c + P], h_rep[:, j, :], ident_f32[:])
+
+            for t in range(TILES):
+                nodes = slice(t * P, (t + 1) * P)
+                e_f32 = work.tile([P, FEATS], F32)
+                for b in range(FEATS // BANK):
+                    cols = slice(b * BANK, (b + 1) * BANK)
+                    nc.vector.tensor_tensor(
+                        out=e_f32[:, cols], in0=e_sb[:, t, cols], in1=h_mean[b][:], op=ALU.add
+                    )
+                squares = work.tile([P, FEATS], BF16)
+                nc.scalar.activation(
+                    out=squares[:], in_=e_f32[:], func=ACT.Square, accum_out=sumsq[:, t : t + 1]
+                )
+                nc.scalar.activation(
+                    out=norm[:, t : t + 1], in_=sumsq[:, t : t + 1], func=ACT.Sqrt, bias=SQRT_GUARD
+                )
+                nc.vector.tensor_scalar(
+                    out=floored[:, t : t + 1],
+                    in0=norm[:, t : t + 1],
+                    scalar1=NORM_FLOOR,
+                    scalar2=None,
+                    op0=ALU.max,
+                )
+                nc.vector.reciprocal(out=inv_norm[:, t : t + 1], in_=floored[:, t : t + 1])
+                e_cur = work.tile([P, FEATS], BF16)
+                nc.gpsimd.tensor_scalar(
+                    out=e_cur[:],
+                    in0=e_f32[:],
+                    scalar1=inv_norm[:, t : t + 1],
+                    scalar2=0.0,
+                    op0=ALU.mult,
+                    op1=ALU.add,
+                )
+                e_t = front_psum.tile([P, BLOCKS, P], BF16, bufs=3)
+                for j in range(BLOCKS):
+                    nc.tensor.transpose(e_t[:, j, :], e_cur[:, j * P : (j + 1) * P], ident_bf16[:])
+                grouped = work.tile([P, PASSES, P, PACK], BF16, align_bytes=64)
+                nc.scalar.copy(
+                    out=grouped[:], in_=e_t[:].rearrange("p (g q) r -> p g r q", q=PACK)
+                )
+                for g in range(PASSES):
+                    nc.vector.quantize_mx(
+                        out=codes[:, g, nodes].bitcast(FP8X4),
+                        scales=scales[:, g, nodes],
+                        in_=grouped[:, g, :, :].rearrange("p r q -> p (r q)"),
+                    )
+
+        with tc.psum_pool(name="back_psum", bufs=1) as back_psum:
+            for i in range(TILES):
+                rows = slice(i * P, (i + 1) * P)
+                for b in range(HALVES):
+                    cols = slice(b * BANK, (b + 1) * BANK)
+                    acc = back_psum.tile([P, BANK], F32, bufs=6)
+                    for g in range(PASSES):
+                        nc.tensor.matmul_mx(
+                            out=acc[:],
+                            lhsT=codes[:, g, rows].bitcast(FP8X4),
+                            lhsT_scale=scales[:, g, rows],
+                            rhs=codes[:, g, cols].bitcast(FP8X4),
+                            rhs_scale=scales[:, g, cols],
+                            start=(g == 0),
+                            stop=(g == PASSES - 1),
+                        )
+                    nc.scalar.activation(
+                        out=g_sb[:, i, cols],
+                        in_=acc[:],
+                        func=ACT.Relu,
+                        accum_out=half_sums[:, i, b : b + 1],
+                    )
+                nc.vector.tensor_reduce(
+                    out=row_sum[:, i : i + 1], in_=half_sums[:, i, :], axis=AXIS.X, op=ALU.add
+                )
+                nc.vector.tensor_scalar(
+                    out=denom[:, i : i + 1],
+                    in0=row_sum[:, i : i + 1],
+                    scalar1=2.0,
+                    scalar2=2.0 * ROWSUM_EPS,
+                    op0=ALU.mult,
+                    op1=ALU.add,
+                )
+                nc.vector.reciprocal(out=w_part[:, i : i + 1], in_=denom[:, i : i + 1])
+                spread = back_psum.tile([P, P], F32, bufs=2)
+                nc.tensor.matmul(
+                    out=spread[:],
+                    lhsT=w_part[:, i : i + 1].to_broadcast([P, P]),
+                    rhs=ident_f32[:],
+                    start=True,
+                    stop=True,
+                )
+                nc.scalar.copy(out=w_free[:, rows], in_=spread[:])
+                if i > 0:
+                    left = slice(0, i * P)
+                    nc.vector.scalar_tensor_tensor(
+                        out=g_sb[:, i, left],
+                        in0=w_free[:, left],
+                        scalar=w_part[:, i : i + 1],
+                        in1=g_sb[:, i, left],
+                        op0=ALU.add,
+                        op1=ALU.mult,
+                    )
+                    nc.sync.dma_start(out=out_rows[:, i, left], in_=g_sb[:, i, left])
+                for r in range(i + 1):
+                    nc.vector.scalar_tensor_tensor(
+                        out=g_sb[:, r, rows],
+                        in0=w_free[:, rows],
+                        scalar=w_part[:, r : r + 1],
+                        in1=g_sb[:, r, rows],
+                        op0=ALU.add,
+                        op1=ALU.mult,
+                    )
+                nc.sync.dma_start(out=out_rows[:, 0 : i + 1, rows], in_=g_sb[:, 0 : i + 1, rows])

@@ -29,6 +29,10 @@ NORM_FLOOR = 1e-12
 ROWSUM_EPS = 1e-6
 SQRT_GUARD = 2.0 ** -110
 
+GROUP = TILES // 2
+INVERT_LAG = 2
+AHEAD = 2
+
 FLOPS = 2 * NODES * NODES * FEATS
 
 
@@ -39,13 +43,14 @@ def tile_gateddynamicfusion_pa_kernel(tc, h_time, E_dyn, out):
     out_rows = out.rearrange("(t p) j -> p t j", p=P)
 
     with ExitStack() as ctx:
+        ctx.enter_context(tc.manual_schedule())
         keep = ctx.enter_context(tc.tile_pool(name="keep", bufs=1))
         work = ctx.enter_context(tc.tile_pool(name="work", bufs=3))
 
         h_sb = keep.tile([P, SLICES, FEATS], BF16)
         e_sb = keep.tile([P, TILES, FEATS], BF16)
-        for s in range(0, SLICES, 2):
-            nc.sync.dma_start(out=h_sb[:, s : s + 2, :], in_=h_rows[:, s : s + 2, :])
+        for s in range(SLICES):
+            nc.sync.dma_start(out=h_sb[:, s, :], in_=h_rows[:, s, :])
         for t in range(0, TILES, 2):
             nc.sync.dma_start(out=e_sb[:, t : t + 2, :], in_=e_rows[:, t : t + 2, :])
 
@@ -60,6 +65,7 @@ def tile_gateddynamicfusion_pa_kernel(tc, h_time, E_dyn, out):
         warm = keep.tile([P, 1], F32)
         nc.scalar.activation(out=warm[:], in_=one[:], func=ACT.Sqrt)
 
+        e_f32 = keep.tile([P, TILES, FEATS], F32)
         codes = keep.tile([P, PASSES, NODES], U32, align_bytes=64)
         scales = keep.tile([P, PASSES, NODES], U8, align_bytes=64)
         g_sb = keep.tile([P, TILES, NODES], F32)
@@ -70,7 +76,7 @@ def tile_gateddynamicfusion_pa_kernel(tc, h_time, E_dyn, out):
         floored = keep.tile([P, TILES], F32)
         inv_norm = keep.tile([P, TILES], F32)
         half_sums = keep.tile([P, TILES, HALVES], F32)
-        row_sum = keep.tile([P, TILES], F32)
+        doubled = keep.tile([P, TILES, HALVES], F32)
         denom = keep.tile([P, TILES], F32)
         w_part = keep.tile([P, TILES], F32)
 
@@ -109,44 +115,59 @@ def tile_gateddynamicfusion_pa_kernel(tc, h_time, E_dyn, out):
                 b, c = divmod(j * P, BANK)
                 nc.tensor.transpose(h_mean[b][:, c : c + P], h_rep[:, j, :], ident_f32[:])
 
-            for t in range(TILES):
-                nodes = slice(t * P, (t + 1) * P)
-                e_f32 = work.tile([P, FEATS], F32)
+            def add_mean(t):
                 for b in range(FEATS // BANK):
                     cols = slice(b * BANK, (b + 1) * BANK)
                     nc.vector.tensor_tensor(
-                        out=e_f32[:, cols], in0=e_sb[:, t, cols], in1=h_mean[b][:], op=ALU.add
+                        out=e_f32[:, t, cols], in0=e_sb[:, t, cols], in1=h_mean[b][:], op=ALU.add
                     )
+
+            def sum_squares(t):
                 squares = work.tile([P, FEATS], BF16)
                 nc.scalar.activation(
-                    out=squares[:], in_=e_f32[:], func=ACT.Square, accum_out=sumsq[:, t : t + 1]
+                    out=squares[:],
+                    in_=e_f32[:, t, :],
+                    func=ACT.Square,
+                    accum_out=sumsq[:, t : t + 1],
                 )
+
+            def roots(tiles):
                 nc.scalar.activation(
-                    out=norm[:, t : t + 1], in_=sumsq[:, t : t + 1], func=ACT.Sqrt, bias=SQRT_GUARD
+                    out=norm[:, tiles], in_=sumsq[:, tiles], func=ACT.Sqrt, bias=SQRT_GUARD
                 )
+
+            def invert(tiles):
                 nc.vector.tensor_scalar(
-                    out=floored[:, t : t + 1],
-                    in0=norm[:, t : t + 1],
+                    out=floored[:, tiles],
+                    in0=norm[:, tiles],
                     scalar1=NORM_FLOOR,
                     scalar2=None,
                     op0=ALU.max,
                 )
-                nc.vector.reciprocal(out=inv_norm[:, t : t + 1], in_=floored[:, t : t + 1])
+                nc.vector.reciprocal(out=inv_norm[:, tiles], in_=floored[:, tiles])
+
+            flipped = {}
+
+            def scale_and_flip(t, engine):
                 e_cur = work.tile([P, FEATS], BF16)
-                nc.gpsimd.tensor_scalar(
+                engine.tensor_scalar(
                     out=e_cur[:],
-                    in0=e_f32[:],
+                    in0=e_f32[:, t, :],
                     scalar1=inv_norm[:, t : t + 1],
                     scalar2=0.0,
                     op0=ALU.mult,
                     op1=ALU.add,
                 )
-                e_t = front_psum.tile([P, BLOCKS, P], BF16, bufs=3)
+                e_t = front_psum.tile([P, BLOCKS, P], BF16, bufs=GROUP + 1)
                 for j in range(BLOCKS):
                     nc.tensor.transpose(e_t[:, j, :], e_cur[:, j * P : (j + 1) * P], ident_bf16[:])
+                flipped[t] = e_t
+
+            def regroup_and_quantise(t):
+                nodes = slice(t * P, (t + 1) * P)
                 grouped = work.tile([P, PASSES, P, PACK], BF16, align_bytes=64)
                 nc.scalar.copy(
-                    out=grouped[:], in_=e_t[:].rearrange("p (g q) r -> p g r q", q=PACK)
+                    out=grouped[:], in_=flipped[t][:].rearrange("p (g q) r -> p g r q", q=PACK)
                 )
                 for g in range(PASSES):
                     nc.vector.quantize_mx(
@@ -155,12 +176,34 @@ def tile_gateddynamicfusion_pa_kernel(tc, h_time, E_dyn, out):
                         in_=grouped[:, g, :, :].rearrange("p r q -> p (r q)"),
                     )
 
+            first = slice(0, GROUP)
+            second = slice(GROUP, TILES)
+            for t in range(TILES):
+                add_mean(t)
+                sum_squares(t)
+                if t == GROUP - 1:
+                    roots(first)
+                if t == GROUP - 1 + INVERT_LAG:
+                    invert(first)
+                    for u in range(GROUP):
+                        scale_and_flip(u, nc.gpsimd)
+            roots(second)
+            invert(second)
+            for u in range(GROUP):
+                scale_and_flip(GROUP + u, nc.vector)
+                regroup_and_quantise(u)
+            for u in range(GROUP):
+                regroup_and_quantise(GROUP + u)
+
         with tc.psum_pool(name="back_psum", bufs=1) as back_psum:
-            for i in range(TILES):
+            sums = {}
+            later = {}
+
+            def products(i):
                 rows = slice(i * P, (i + 1) * P)
                 for b in range(HALVES):
                     cols = slice(b * BANK, (b + 1) * BANK)
-                    acc = back_psum.tile([P, BANK], F32, bufs=6)
+                    acc = back_psum.tile([P, BANK], F32, bufs=(AHEAD + 1) * HALVES)
                     for g in range(PASSES):
                         nc.tensor.matmul_mx(
                             out=acc[:],
@@ -171,51 +214,61 @@ def tile_gateddynamicfusion_pa_kernel(tc, h_time, E_dyn, out):
                             start=(g == 0),
                             stop=(g == PASSES - 1),
                         )
-                    nc.scalar.activation(
-                        out=g_sb[:, i, cols],
-                        in_=acc[:],
-                        func=ACT.Relu,
-                        accum_out=half_sums[:, i, b : b + 1],
-                    )
-                nc.vector.tensor_reduce(
-                    out=row_sum[:, i : i + 1], in_=half_sums[:, i, :], axis=AXIS.X, op=ALU.add
-                )
-                nc.vector.tensor_scalar(
-                    out=denom[:, i : i + 1],
-                    in0=row_sum[:, i : i + 1],
-                    scalar1=2.0,
-                    scalar2=2.0 * ROWSUM_EPS,
-                    op0=ALU.mult,
-                    op1=ALU.add,
-                )
-                nc.vector.reciprocal(out=w_part[:, i : i + 1], in_=denom[:, i : i + 1])
-                spread = back_psum.tile([P, P], F32, bufs=2)
+                    sums[(i, b)] = acc
+
+            def spread(i, name):
+                w_bank = back_psum.tile([P, P], F32, name=name)
                 nc.tensor.matmul(
-                    out=spread[:],
+                    out=w_bank[:],
                     lhsT=w_part[:, i : i + 1].to_broadcast([P, P]),
                     rhs=ident_f32[:],
                     start=True,
                     stop=True,
                 )
-                nc.scalar.copy(out=w_free[:, rows], in_=spread[:])
+                return w_bank
+
+            def finish(r, cols, w_cols):
+                nc.vector.scalar_tensor_tensor(
+                    out=g_sb[:, r, cols],
+                    in0=w_cols,
+                    scalar=w_part[:, r : r + 1],
+                    in1=g_sb[:, r, cols],
+                    op0=ALU.add,
+                    op1=ALU.mult,
+                )
+
+            for i in range(AHEAD):
+                products(i)
+            for i in range(TILES):
+                rows = slice(i * P, (i + 1) * P)
+                if i + AHEAD < TILES:
+                    products(i + AHEAD)
+                for b in range(HALVES):
+                    nc.scalar.activation(
+                        out=g_sb[:, i, b * BANK : (b + 1) * BANK],
+                        in_=sums[(i, b)][:],
+                        func=ACT.Relu,
+                        accum_out=half_sums[:, i, b : b + 1],
+                    )
+                if i > 0:
+                    nc.scalar.copy(out=w_free[:, (i - 1) * P : i * P], in_=later[i - 1][:])
+                nc.vector.tensor_scalar(
+                    out=doubled[:, i, :],
+                    in0=half_sums[:, i, :],
+                    scalar1=2.0,
+                    scalar2=2.0 * ROWSUM_EPS,
+                    op0=ALU.mult,
+                    op1=ALU.add,
+                    accum_out=denom[:, i : i + 1],
+                )
+                nc.vector.reciprocal(out=w_part[:, i : i + 1], in_=denom[:, i : i + 1])
+                w_now = spread(i, "w_now")
                 if i > 0:
                     left = slice(0, i * P)
-                    nc.vector.scalar_tensor_tensor(
-                        out=g_sb[:, i, left],
-                        in0=w_free[:, left],
-                        scalar=w_part[:, i : i + 1],
-                        in1=g_sb[:, i, left],
-                        op0=ALU.add,
-                        op1=ALU.mult,
-                    )
+                    finish(i, left, w_free[:, left])
                     nc.sync.dma_start(out=out_rows[:, i, left], in_=g_sb[:, i, left])
                 for r in range(i + 1):
-                    nc.vector.scalar_tensor_tensor(
-                        out=g_sb[:, r, rows],
-                        in0=w_free[:, rows],
-                        scalar=w_part[:, r : r + 1],
-                        in1=g_sb[:, r, rows],
-                        op0=ALU.add,
-                        op1=ALU.mult,
-                    )
+                    finish(r, rows, w_now[:])
                 nc.sync.dma_start(out=out_rows[:, 0 : i + 1, rows], in_=g_sb[:, 0 : i + 1, rows])
+                if i + 1 < TILES:
+                    later[i] = spread(i, "w_later")

@@ -69,7 +69,6 @@ def tile_gateddynamicfusion_pa_kernel(tc, h_time, E_dyn, out):
         codes = keep.tile([P, PASSES, NODES], U32, align_bytes=64)
         scales = keep.tile([P, PASSES, NODES], U8, align_bytes=64)
         g_sb = keep.tile([P, TILES, NODES], F32)
-        w_free = keep.tile([P, NODES], F32)
 
         sumsq = keep.tile([P, TILES], F32)
         norm = keep.tile([P, TILES], F32)
@@ -197,7 +196,7 @@ def tile_gateddynamicfusion_pa_kernel(tc, h_time, E_dyn, out):
 
         with tc.psum_pool(name="back_psum", bufs=1) as back_psum:
             sums = {}
-            later = {}
+            w_free = [back_psum.tile([P, BANK], F32, name="w_free%d" % b) for b in range(HALVES)]
 
             def products(i):
                 rows = slice(i * P, (i + 1) * P)
@@ -216,21 +215,11 @@ def tile_gateddynamicfusion_pa_kernel(tc, h_time, E_dyn, out):
                         )
                     sums[(i, b)] = acc
 
-            def spread(i, name):
-                w_bank = back_psum.tile([P, P], F32, name=name)
-                nc.tensor.matmul(
-                    out=w_bank[:],
-                    lhsT=w_part[:, i : i + 1].to_broadcast([P, P]),
-                    rhs=ident_f32[:],
-                    start=True,
-                    stop=True,
-                )
-                return w_bank
-
-            def finish(r, cols, w_cols):
+            def finish(r, b, lo, hi):
+                cols = slice(b * BANK + lo, b * BANK + hi)
                 nc.vector.scalar_tensor_tensor(
                     out=g_sb[:, r, cols],
-                    in0=w_cols,
+                    in0=w_free[b][:, lo:hi],
                     scalar=w_part[:, r : r + 1],
                     in1=g_sb[:, r, cols],
                     op0=ALU.add,
@@ -240,7 +229,6 @@ def tile_gateddynamicfusion_pa_kernel(tc, h_time, E_dyn, out):
             for i in range(AHEAD):
                 products(i)
             for i in range(TILES):
-                rows = slice(i * P, (i + 1) * P)
                 if i + AHEAD < TILES:
                     products(i + AHEAD)
                 for b in range(HALVES):
@@ -250,8 +238,6 @@ def tile_gateddynamicfusion_pa_kernel(tc, h_time, E_dyn, out):
                         func=ACT.Relu,
                         accum_out=half_sums[:, i, b : b + 1],
                     )
-                if i > 0:
-                    nc.scalar.copy(out=w_free[:, (i - 1) * P : i * P], in_=later[i - 1][:])
                 nc.vector.tensor_scalar(
                     out=doubled[:, i, :],
                     in0=half_sums[:, i, :],
@@ -262,13 +248,23 @@ def tile_gateddynamicfusion_pa_kernel(tc, h_time, E_dyn, out):
                     accum_out=denom[:, i : i + 1],
                 )
                 nc.vector.reciprocal(out=w_part[:, i : i + 1], in_=denom[:, i : i + 1])
-                w_now = spread(i, "w_now")
+                bank, lo = divmod(i * P, BANK)
+                nc.tensor.matmul(
+                    out=w_free[bank][:, lo : lo + P],
+                    lhsT=w_part[:, i : i + 1].to_broadcast([P, P]),
+                    rhs=ident_f32[:],
+                    start=True,
+                    stop=True,
+                )
+                for b in range(bank):
+                    finish(i, b, 0, BANK)
+                    full = slice(b * BANK, (b + 1) * BANK)
+                    nc.sync.dma_start(out=out_rows[:, i, full], in_=g_sb[:, i, full])
+                for r in range(i):
+                    finish(r, bank, lo, lo + P)
                 if i > 0:
-                    left = slice(0, i * P)
-                    finish(i, left, w_free[:, left])
-                    nc.sync.dma_start(out=out_rows[:, i, left], in_=g_sb[:, i, left])
-                for r in range(i + 1):
-                    finish(r, rows, w_now[:])
-                nc.sync.dma_start(out=out_rows[:, 0 : i + 1, rows], in_=g_sb[:, 0 : i + 1, rows])
-                if i + 1 < TILES:
-                    later[i] = spread(i, "w_later")
+                    above = slice(i * P, (i + 1) * P)
+                    nc.sync.dma_start(out=out_rows[:, 0:i, above], in_=g_sb[:, 0:i, above])
+                finish(i, bank, 0, lo + P)
+                rest = slice(bank * BANK, (i + 1) * P)
+                nc.sync.dma_start(out=out_rows[:, i, rest], in_=g_sb[:, i, rest])

@@ -22,6 +22,7 @@ BLOCKS = FEATS // P
 PACK = 4
 PASSES = FEATS // (P * PACK)
 BANK = 512
+PSUM_BANKS = 8
 HALVES = NODES // BANK
 ONES = 8
 
@@ -31,6 +32,7 @@ SQRT_GUARD = 2.0 ** -110
 
 GROUP = TILES // 2
 INVERT_LAG = 2
+VECTOR_REGROUPS = 1
 AHEAD = 2
 
 FLOPS = 2 * NODES * NODES * FEATS
@@ -62,10 +64,13 @@ def tile_gateddynamicfusion_pa_kernel(tc, h_time, E_dyn, out):
         nc.vector.memset(ones[:], 1.0)
         one = keep.tile([P, 1], F32)
         nc.vector.memset(one[:], 1.0)
+        minus_one = keep.tile([P, 1], F32)
+        nc.vector.memset(minus_one[:], -1.0)
         warm = keep.tile([P, 1], F32)
         nc.scalar.activation(out=warm[:], in_=one[:], func=ACT.Sqrt)
 
         e_f32 = keep.tile([P, TILES, FEATS], F32)
+        grouped = keep.tile([P, TILES, PASSES, P, PACK], BF16, align_bytes=64)
         codes = keep.tile([P, PASSES, NODES], U32, align_bytes=64)
         scales = keep.tile([P, PASSES, NODES], U8, align_bytes=64)
         g_sb = keep.tile([P, TILES, NODES], F32)
@@ -79,8 +84,8 @@ def tile_gateddynamicfusion_pa_kernel(tc, h_time, E_dyn, out):
         denom = keep.tile([P, TILES], F32)
         w_part = keep.tile([P, TILES], F32)
 
-        with tc.psum_pool(name="front_psum", bufs=1) as front_psum:
-            h_part = front_psum.tile([P, BLOCKS, SLICES, ONES], F32)
+        with tc.psum_pool(name="front_psum", bufs=PSUM_BANKS) as front_psum:
+            h_part = front_psum.tile([P, BLOCKS, SLICES, ONES], F32, tag="bank")
             for s in range(SLICES):
                 for j in range(BLOCKS):
                     nc.tensor.matmul(
@@ -108,7 +113,8 @@ def tile_gateddynamicfusion_pa_kernel(tc, h_time, E_dyn, out):
                 scale=1.0 / H_ROWS,
             )
             h_mean = [
-                front_psum.tile([P, BANK], F32, name="h_mean%d" % b) for b in range(FEATS // BANK)
+                front_psum.tile([P, BANK], F32, name="h_mean%d" % b, tag="bank")
+                for b in range(FEATS // BANK)
             ]
             for j in range(BLOCKS):
                 b, c = divmod(j * P, BANK)
@@ -157,22 +163,24 @@ def tile_gateddynamicfusion_pa_kernel(tc, h_time, E_dyn, out):
                     op0=ALU.mult,
                     op1=ALU.add,
                 )
-                e_t = front_psum.tile([P, BLOCKS, P], BF16, bufs=GROUP + 1)
+                e_t = front_psum.tile([P, BLOCKS, P], BF16, tag="bank")
                 for j in range(BLOCKS):
                     nc.tensor.transpose(e_t[:, j, :], e_cur[:, j * P : (j + 1) * P], ident_bf16[:])
                 flipped[t] = e_t
 
-            def regroup_and_quantise(t):
-                nodes = slice(t * P, (t + 1) * P)
-                grouped = work.tile([P, PASSES, P, PACK], BF16, align_bytes=64)
-                nc.scalar.copy(
-                    out=grouped[:], in_=flipped[t][:].rearrange("p (g q) r -> p g r q", q=PACK)
+            def regroup(t, copy):
+                copy(
+                    out=grouped[:, t, :, :, :],
+                    in_=flipped[t][:].rearrange("p (g q) r -> p g r q", q=PACK),
                 )
+
+            def quantise(t):
+                nodes = slice(t * P, (t + 1) * P)
                 for g in range(PASSES):
                     nc.vector.quantize_mx(
                         out=codes[:, g, nodes].bitcast(FP8X4),
                         scales=scales[:, g, nodes],
-                        in_=grouped[:, g, :, :].rearrange("p r q -> p (r q)"),
+                        in_=grouped[:, t, g, :, :].rearrange("p r q -> p (r q)"),
                     )
 
             first = slice(0, GROUP)
@@ -188,11 +196,16 @@ def tile_gateddynamicfusion_pa_kernel(tc, h_time, E_dyn, out):
                         scale_and_flip(u, nc.gpsimd)
             roots(second)
             invert(second)
-            for u in range(GROUP):
-                scale_and_flip(GROUP + u, nc.vector)
-                regroup_and_quantise(u)
-            for u in range(GROUP):
-                regroup_and_quantise(GROUP + u)
+            for t in range(GROUP, TILES):
+                scale_and_flip(t, nc.vector)
+            for t in range(TILES):
+                if GROUP - VECTOR_REGROUPS <= t < GROUP:
+                    regroup(t, nc.vector.tensor_copy)
+                else:
+                    regroup(t, nc.scalar.copy)
+                if t > 0:
+                    quantise(t - 1)
+            quantise(TILES - 1)
 
         with tc.psum_pool(name="back_psum", bufs=1) as back_psum:
             sums = {}
@@ -238,16 +251,23 @@ def tile_gateddynamicfusion_pa_kernel(tc, h_time, E_dyn, out):
                         func=ACT.Relu,
                         accum_out=half_sums[:, i, b : b + 1],
                     )
-                nc.vector.tensor_scalar(
+                nc.gpsimd.tensor_scalar(
                     out=doubled[:, i, :],
                     in0=half_sums[:, i, :],
                     scalar1=2.0,
-                    scalar2=2.0 * ROWSUM_EPS,
+                    scalar2=ROWSUM_EPS,
                     op0=ALU.mult,
                     op1=ALU.add,
-                    accum_out=denom[:, i : i + 1],
                 )
-                nc.vector.reciprocal(out=w_part[:, i : i + 1], in_=denom[:, i : i + 1])
+                nc.gpsimd.tensor_tensor(
+                    out=denom[:, i : i + 1],
+                    in0=doubled[:, i, 0:1],
+                    in1=doubled[:, i, 1:2],
+                    op=ALU.add,
+                )
+                nc.gpsimd.tensor_tensor(
+                    out=w_part[:, i : i + 1], in0=denom[:, i : i + 1], in1=minus_one[:], op=ALU.pow
+                )
                 bank, lo = divmod(i * P, BANK)
                 nc.tensor.matmul(
                     out=w_free[bank][:, lo : lo + P],

@@ -20,20 +20,30 @@ TILES = NODES // P
 SLICES = H_ROWS // P
 BLOCKS = FEATS // P
 PACK = 4
+PAIRS = PACK // 2
 PASSES = FEATS // (P * PACK)
 BANK = 512
 PSUM_BANKS = 8
+BANK_BYTES = 4 * BANK
 HALVES = NODES // BANK
+RING_START = HALVES
+RING = PSUM_BANKS - RING_START
 ONES = 8
+COLUMN_SLICES = (1, 2, 3)
+SLICES_BEFORE_JOIN = 5
 
 NORM_FLOOR = 1e-12
 ROWSUM_EPS = 1e-6
 SQRT_GUARD = 2.0 ** -110
 
-GROUP = TILES // 2
+NORM_GROUPS = (slice(0, 1), slice(1, 2), slice(2, 4), slice(4, 6), slice(6, 8))
 INVERT_LAG = 2
-VECTOR_REGROUPS = 1
-AHEAD = 2
+SCALED_BY_VECTOR = (6, 7)
+REGROUPED_BY_VECTOR = (0, 1)
+RELU_BY_VECTOR = ((0, 1), (1, 1))
+AHEAD = 3
+MIRRORED = (5, 6, 7)
+WARM_UPS = 2
 
 FLOPS = 2 * NODES * NODES * FEATS
 
@@ -53,15 +63,15 @@ def tile_gateddynamicfusion_pa_kernel(tc, h_time, E_dyn, out):
         e_sb = keep.tile([P, TILES, FEATS], BF16)
         for s in range(SLICES):
             nc.sync.dma_start(out=h_sb[:, s, :], in_=h_rows[:, s, :])
-        for t in range(0, TILES, 2):
-            nc.sync.dma_start(out=e_sb[:, t : t + 2, :], in_=e_rows[:, t : t + 2, :])
+        for t in range(TILES):
+            nc.sync.dma_start(out=e_sb[:, t, :], in_=e_rows[:, t, :])
 
         ident_f32 = keep.tile([P, P], F32)
         make_identity(nc, ident_f32[:])
-        ident_bf16 = keep.tile([P, P], BF16)
-        make_identity(nc, ident_bf16[:])
-        ones = keep.tile([P, ONES], BF16)
-        nc.vector.memset(ones[:], 1.0)
+        zeros = keep.tile([P, BANK], BF16)
+        nc.vector.memset(zeros[:], 0.0)
+        ones = keep.tile([P, P], BF16)
+        nc.vector.memset(ones[:], 1.0 / H_ROWS)
         one = keep.tile([P, 1], F32)
         nc.vector.memset(one[:], 1.0)
         minus_one = keep.tile([P, 1], F32)
@@ -80,52 +90,73 @@ def tile_gateddynamicfusion_pa_kernel(tc, h_time, E_dyn, out):
         floored = keep.tile([P, TILES], F32)
         inv_norm = keep.tile([P, TILES], F32)
         half_sums = keep.tile([P, TILES, HALVES], F32)
-        doubled = keep.tile([P, TILES, HALVES], F32)
+        doubled = keep.tile([P, TILES], F32)
         denom = keep.tile([P, TILES], F32)
         w_part = keep.tile([P, TILES], F32)
 
-        with tc.psum_pool(name="front_psum", bufs=PSUM_BANKS) as front_psum:
-            h_part = front_psum.tile([P, BLOCKS, SLICES, ONES], F32, tag="bank")
-            for s in range(SLICES):
+        psum = ctx.enter_context(tc.psum_pool(name="psum", bufs=1))
+
+        def bank_tile(name, bank, shape):
+            return psum.tile(shape, F32, name=name, offset=bank * BANK_BYTES)
+
+        with ExitStack():
+            h_part = bank_tile("h_part", RING_START, [P, BLOCKS, len(COLUMN_SLICES), ONES])
+            idle = bank_tile("idle", RING_START + 1, [P, BANK])
+            h_mean = [bank_tile("h_mean%d" % b, b, [P, BANK]) for b in range(FEATS // BANK)]
+            h_sum = keep.tile([P, BLOCKS], F32)
+
+            def spread_slice(s, b):
+                nc.tensor.matmul(
+                    out=h_mean[b][:],
+                    lhsT=ones[:],
+                    rhs=h_sb[:, s, b * BANK : (b + 1) * BANK],
+                    start=(s == 0),
+                    stop=(s == SLICES - 1),
+                )
+
+            def sum_slice(s):
                 for j in range(BLOCKS):
                     nc.tensor.matmul(
-                        out=h_part[:, j, s, :],
+                        out=h_part[:, j, COLUMN_SLICES.index(s), :],
                         lhsT=h_sb[:, s, j * P : (j + 1) * P],
-                        rhs=ones[:],
+                        rhs=ones[:, 0:ONES],
                         start=True,
                         stop=True,
                     )
-            h_sum = keep.tile([P, BLOCKS], F32)
-            nc.vector.tensor_reduce(out=h_sum[:], in_=h_part[:, :, :, 0], axis=AXIS.X, op=ALU.add)
-            h_rep = keep.tile([P, BLOCKS, P], F32)
-            half = BLOCKS // 2
-            nc.vector.tensor_scalar(
-                out=h_rep[:, 0:half, :],
-                in0=h_sum[:, 0:half].unsqueeze(2).to_broadcast([P, half, P]),
-                scalar1=1.0 / H_ROWS,
-                scalar2=None,
-                op0=ALU.mult,
-            )
-            nc.scalar.activation(
-                out=h_rep[:, half:BLOCKS, :],
-                in_=h_sum[:, half:BLOCKS].unsqueeze(2).to_broadcast([P, half, P]),
-                func=ACT.Copy,
-                scale=1.0 / H_ROWS,
-            )
-            h_mean = [
-                front_psum.tile([P, BANK], F32, name="h_mean%d" % b, tag="bank")
-                for b in range(FEATS // BANK)
-            ]
-            for j in range(BLOCKS):
-                b, c = divmod(j * P, BANK)
-                nc.tensor.transpose(h_mean[b][:, c : c + P], h_rep[:, j, :], ident_f32[:])
 
-            def add_mean(t):
-                for b in range(FEATS // BANK):
-                    cols = slice(b * BANK, (b + 1) * BANK)
-                    nc.vector.tensor_tensor(
-                        out=e_f32[:, t, cols], in0=e_sb[:, t, cols], in1=h_mean[b][:], op=ALU.add
+            def join_sums(b):
+                for c in range(0, BANK, P):
+                    j = (b * BANK + c) // P
+                    nc.tensor.matmul(
+                        out=h_mean[b][:, c : c + P],
+                        lhsT=h_sum[:, j : j + 1].to_broadcast([P, P]),
+                        rhs=ident_f32[:],
+                        start=False,
+                        stop=False,
+                        is_transpose=True,
                     )
+
+            for n in range(WARM_UPS):
+                nc.tensor.matmul(
+                    out=idle[:], lhsT=zeros[:, 0:P], rhs=zeros[:], start=True, stop=True
+                )
+            for s in range(SLICES_BEFORE_JOIN):
+                if s in COLUMN_SLICES:
+                    sum_slice(s)
+                else:
+                    for b in range(FEATS // BANK):
+                        spread_slice(s, b)
+            nc.vector.tensor_reduce(out=h_sum[:], in_=h_part[:, :, :, 0], axis=AXIS.X, op=ALU.add)
+            for b in range(FEATS // BANK):
+                join_sums(b)
+                for s in range(SLICES_BEFORE_JOIN, SLICES):
+                    spread_slice(s, b)
+
+            def add_mean(t, b):
+                cols = slice(b * BANK, (b + 1) * BANK)
+                nc.vector.tensor_tensor(
+                    out=e_f32[:, t, cols], in0=e_sb[:, t, cols], in1=h_mean[b][:], op=ALU.add
+                )
 
             def sum_squares(t):
                 squares = work.tile([P, FEATS], BF16)
@@ -153,25 +184,29 @@ def tile_gateddynamicfusion_pa_kernel(tc, h_time, E_dyn, out):
 
             flipped = {}
 
-            def scale_and_flip(t, engine):
-                e_cur = work.tile([P, FEATS], BF16)
+            def scale_and_flip(t):
+                engine = nc.vector if t in SCALED_BY_VECTOR else nc.gpsimd
+                e_cur = work.tile([P, FEATS], BF16, bufs=4)
                 engine.tensor_scalar(
-                    out=e_cur[:],
-                    in0=e_f32[:, t, :],
+                    out=e_cur[:].rearrange("p (u w e) -> p u w e", u=PAIRS, e=2),
+                    in0=e_f32[:, t, :].rearrange("p (w u e) -> p u w e", u=PAIRS, e=2),
                     scalar1=inv_norm[:, t : t + 1],
                     scalar2=0.0,
                     op0=ALU.mult,
                     op1=ALU.add,
                 )
-                e_t = front_psum.tile([P, BLOCKS, P], BF16, tag="bank")
-                for j in range(BLOCKS):
-                    nc.tensor.transpose(e_t[:, j, :], e_cur[:, j * P : (j + 1) * P], ident_bf16[:])
+                words = e_cur[:].bitcast(F32).rearrange("p (u g q) -> p u g q", u=PAIRS, g=PASSES)
+                e_t = bank_tile("e_t%d" % t, RING_START + t % RING, [P, PASSES, PAIRS, P])
+                for g in range(PASSES):
+                    for u in range(PAIRS):
+                        nc.tensor.transpose(e_t[:, g, u, :], words[:, u, g, :], ident_f32[:])
                 flipped[t] = e_t
 
-            def regroup(t, copy):
+            def regroup(t):
+                copy = nc.vector.tensor_copy if t in REGROUPED_BY_VECTOR else nc.scalar.copy
                 copy(
-                    out=grouped[:, t, :, :, :],
-                    in_=flipped[t][:].rearrange("p (g q) r -> p g r q", q=PACK),
+                    out=grouped[:, t, :, :, :].bitcast(F32),
+                    in_=flipped[t][:].rearrange("p g u r -> p g r u"),
                 )
 
             def quantise(t):
@@ -183,108 +218,153 @@ def tile_gateddynamicfusion_pa_kernel(tc, h_time, E_dyn, out):
                         in_=grouped[:, t, g, :, :].rearrange("p r q -> p (r q)"),
                     )
 
-            first = slice(0, GROUP)
-            second = slice(GROUP, TILES)
             for t in range(TILES):
-                add_mean(t)
+                for b in range(FEATS // BANK):
+                    add_mean(t, b)
+                for group in NORM_GROUPS:
+                    if t == min(group.stop - 1 + INVERT_LAG, TILES - 1) and group.stop < TILES:
+                        invert(group)
+                        for u in range(group.start, group.stop):
+                            scale_and_flip(u)
                 sum_squares(t)
-                if t == GROUP - 1:
-                    roots(first)
-                if t == GROUP - 1 + INVERT_LAG:
-                    invert(first)
-                    for u in range(GROUP):
-                        scale_and_flip(u, nc.gpsimd)
-            roots(second)
-            invert(second)
-            for t in range(GROUP, TILES):
-                scale_and_flip(t, nc.vector)
-            for t in range(TILES):
-                if GROUP - VECTOR_REGROUPS <= t < GROUP:
-                    regroup(t, nc.vector.tensor_copy)
-                else:
-                    regroup(t, nc.scalar.copy)
-                if t > 0:
-                    quantise(t - 1)
-            quantise(TILES - 1)
+                for group in NORM_GROUPS:
+                    if t == group.stop - 1:
+                        roots(group)
+            for t in range(2):
+                regroup(t)
+            for t in range(2):
+                quantise(t)
+            invert(group)
+            for t in range(group.start, group.stop):
+                scale_and_flip(t)
+            for t in range(2, TILES):
+                regroup(t)
+            for t in range(2, TILES):
+                quantise(t)
 
-        with tc.psum_pool(name="back_psum", bufs=1) as back_psum:
-            sums = {}
-            w_free = [back_psum.tile([P, BANK], F32, name="w_free%d" % b) for b in range(HALVES)]
+        sums = {}
+        w_free = [bank_tile("w_free%d" % b, b, [P, BANK]) for b in range(HALVES)]
 
-            def products(i):
-                rows = slice(i * P, (i + 1) * P)
-                for b in range(HALVES):
-                    cols = slice(b * BANK, (b + 1) * BANK)
-                    acc = back_psum.tile([P, BANK], F32, bufs=(AHEAD + 1) * HALVES)
-                    for g in range(PASSES):
-                        nc.tensor.matmul_mx(
-                            out=acc[:],
-                            lhsT=codes[:, g, rows].bitcast(FP8X4),
-                            lhsT_scale=scales[:, g, rows],
-                            rhs=codes[:, g, cols].bitcast(FP8X4),
-                            rhs_scale=scales[:, g, cols],
-                            start=(g == 0),
-                            stop=(g == PASSES - 1),
-                        )
-                    sums[(i, b)] = acc
+        FIRST = TILES // HALVES
+        order = [(i, 0) for i in range(FIRST)] + [(i, 1) for i in range(FIRST)]
+        for i in range(FIRST, TILES):
+            order += [(i, 0), (i, 1)]
 
-            def finish(r, b, lo, hi):
-                cols = slice(b * BANK + lo, b * BANK + hi)
-                nc.vector.scalar_tensor_tensor(
-                    out=g_sb[:, r, cols],
-                    in0=w_free[b][:, lo:hi],
-                    scalar=w_part[:, r : r + 1],
-                    in1=g_sb[:, r, cols],
-                    op0=ALU.add,
-                    op1=ALU.mult,
+        def products(n):
+            i, b = order[n]
+            rows = slice(i * P, (i + 1) * P)
+            cols = slice(b * BANK, (b + 1) * BANK)
+            acc = bank_tile("acc%d" % n, RING_START + (TILES + n) % RING, [P, BANK])
+            for g in range(PASSES):
+                nc.tensor.matmul_mx(
+                    out=acc[:],
+                    lhsT=codes[:, g, rows].bitcast(FP8X4),
+                    lhsT_scale=scales[:, g, rows],
+                    rhs=codes[:, g, cols].bitcast(FP8X4),
+                    rhs_scale=scales[:, g, cols],
+                    start=(g == 0),
+                    stop=(g == PASSES - 1),
                 )
+            sums[n] = acc
 
-            for i in range(AHEAD):
-                products(i)
-            for i in range(TILES):
-                if i + AHEAD < TILES:
-                    products(i + AHEAD)
-                for b in range(HALVES):
-                    nc.scalar.activation(
-                        out=g_sb[:, i, b * BANK : (b + 1) * BANK],
-                        in_=sums[(i, b)][:],
-                        func=ACT.Relu,
-                        accum_out=half_sums[:, i, b : b + 1],
-                    )
+        def finish(r, b, lo, hi):
+            cols = slice(b * BANK + lo, b * BANK + hi)
+            nc.vector.scalar_tensor_tensor(
+                out=g_sb[:, r, cols],
+                in0=w_free[b][:, lo:hi],
+                scalar=w_part[:, r : r + 1],
+                in1=g_sb[:, r, cols],
+                op0=ALU.add,
+                op1=ALU.mult,
+            )
+
+        def relu(n):
+            i, b = order[n]
+            half = g_sb[:, i, b * BANK : (b + 1) * BANK]
+            half_sum = half_sums[:, i, b : b + 1]
+            if (i, b) in RELU_BY_VECTOR:
+                nc.vector.tensor_scalar(
+                    out=half,
+                    in0=sums[n][:],
+                    scalar1=0.0,
+                    scalar2=0.0,
+                    op0=ALU.max,
+                    op1=ALU.add,
+                    accum_out=half_sum,
+                )
+            else:
+                nc.scalar.activation(out=half, in_=sums[n][:], func=ACT.Relu, accum_out=half_sum)
+            if b == 0:
                 nc.gpsimd.tensor_scalar(
-                    out=doubled[:, i, :],
-                    in0=half_sums[:, i, :],
+                    out=doubled[:, i : i + 1],
+                    in0=half_sums[:, i, 0:1],
                     scalar1=2.0,
-                    scalar2=ROWSUM_EPS,
+                    scalar2=2.0 * ROWSUM_EPS,
                     op0=ALU.mult,
                     op1=ALU.add,
                 )
-                nc.gpsimd.tensor_tensor(
+            else:
+                engine = nc.vector if i == TILES - 1 else nc.gpsimd
+                engine.tensor_scalar(
                     out=denom[:, i : i + 1],
-                    in0=doubled[:, i, 0:1],
-                    in1=doubled[:, i, 1:2],
-                    op=ALU.add,
+                    in0=half_sums[:, i, 1:2],
+                    scalar1=2.0,
+                    scalar2=doubled[:, i : i + 1],
+                    op0=ALU.mult,
+                    op1=ALU.add,
                 )
-                nc.gpsimd.tensor_tensor(
-                    out=w_part[:, i : i + 1], in0=denom[:, i : i + 1], in1=minus_one[:], op=ALU.pow
-                )
-                bank, lo = divmod(i * P, BANK)
-                nc.tensor.matmul(
-                    out=w_free[bank][:, lo : lo + P],
-                    lhsT=w_part[:, i : i + 1].to_broadcast([P, P]),
-                    rhs=ident_f32[:],
-                    start=True,
-                    stop=True,
-                )
-                for b in range(bank):
-                    finish(i, b, 0, BANK)
-                    full = slice(b * BANK, (b + 1) * BANK)
-                    nc.sync.dma_start(out=out_rows[:, i, full], in_=g_sb[:, i, full])
+                if i == TILES - 1:
+                    nc.vector.reciprocal(out=w_part[:, i : i + 1], in_=denom[:, i : i + 1])
+                else:
+                    nc.gpsimd.tensor_tensor(
+                        out=w_part[:, i : i + 1],
+                        in0=denom[:, i : i + 1],
+                        in1=minus_one[:],
+                        op=ALU.pow,
+                    )
+
+        def complete(i):
+            bank, lo = divmod(i * P, BANK)
+            nc.tensor.transpose(
+                w_free[bank][:, lo : lo + P],
+                w_part[:, i : i + 1].to_broadcast([P, P]),
+                ident_f32[:],
+            )
+            for b in range(bank):
+                finish(i, b, 0, BANK)
+                full = slice(b * BANK, (b + 1) * BANK)
+                nc.sync.dma_start(out=out_rows[:, i, full], in_=g_sb[:, i, full])
+            if i > 0 and i not in MIRRORED:
                 for r in range(i):
                     finish(r, bank, lo, lo + P)
-                if i > 0:
-                    above = slice(i * P, (i + 1) * P)
-                    nc.sync.dma_start(out=out_rows[:, 0:i, above], in_=g_sb[:, 0:i, above])
-                finish(i, bank, 0, lo + P)
-                rest = slice(bank * BANK, (i + 1) * P)
-                nc.sync.dma_start(out=out_rows[:, i, rest], in_=g_sb[:, i, rest])
+                above = slice(i * P, (i + 1) * P)
+                nc.sync.dma_start(out=out_rows[:, 0:i, above], in_=g_sb[:, 0:i, above])
+            finish(i, bank, 0, lo + P)
+            rest = slice(bank * BANK, (i + 1) * P)
+            nc.sync.dma_start(out=out_rows[:, i, rest], in_=g_sb[:, i, rest])
+
+        def mirror(i):
+            above = slice(i * P, (i + 1) * P)
+            for r in range(0, i, BANK // P):
+                tiles = slice(r, min(r + BANK // P, i))
+                count = tiles.stop - tiles.start
+                m_t = bank_tile("m_t%d_%d" % (i, r), RING_START + (i * HALVES + r // 4) % RING, [P, BANK // P, P])
+                for q in range(count):
+                    nc.tensor.transpose(
+                        m_t[:, q, :], g_sb[:, i, (r + q) * P : (r + q + 1) * P], ident_f32[:]
+                    )
+                nc.scalar.copy(out=g_sb[:, tiles, above], in_=m_t[:, 0:count, :])
+                nc.sync.dma_start(out=out_rows[:, tiles, above], in_=g_sb[:, tiles, above])
+
+        units = len(order)
+        for n in range(AHEAD):
+            products(n)
+        for n in range(units):
+            relu(n)
+            if n + AHEAD < units:
+                products(n + AHEAD)
+            if n > 0 and order[n - 1][1] == HALVES - 1:
+                complete(order[n - 1][0])
+        complete(TILES - 1)
+        for i in MIRRORED:
+            mirror(i)

@@ -28,22 +28,22 @@ BANK_BYTES = 4 * BANK
 HALVES = NODES // BANK
 RING_START = HALVES
 RING = PSUM_BANKS - RING_START
-ONES = 8
-COLUMN_SLICES = (1, 2, 3)
-SLICES_BEFORE_JOIN = 5
+ONES = 2
+COLUMN_SLICES = (1, 2, 4, 5)
+SLICES_BEFORE_JOIN = 7
 
 NORM_FLOOR = 1e-12
 ROWSUM_EPS = 1e-6
 SQRT_GUARD = 2.0 ** -110
 
-NORM_GROUPS = (slice(0, 1), slice(1, 2), slice(2, 4), slice(4, 6), slice(6, 8))
+NORM_GROUPS = (slice(0, 2), slice(2, 4), slice(4, 6), slice(6, 8))
 INVERT_LAG = 2
-SCALED_BY_VECTOR = (6, 7)
+SCALED_BY_VECTOR = (4, 7)
 REGROUPED_BY_VECTOR = (0, 1)
-RELU_BY_VECTOR = ((0, 1), (1, 1))
-AHEAD = 3
-MIRRORED = (5, 6, 7)
-WARM_UPS = 2
+RELU_BY_VECTOR = ((3, 0), (0, 1), (1, 1))
+AHEAD = 2
+WARM_UPS = 4
+WARM_AFTER = {1: (7, 2), 2: (7, 2), 4: (1, 1), 5: (1, 1)}
 
 FLOPS = 2 * NODES * NODES * FEATS
 
@@ -68,7 +68,7 @@ def tile_gateddynamicfusion_pa_kernel(tc, h_time, E_dyn, out):
 
         ident_f32 = keep.tile([P, P], F32)
         make_identity(nc, ident_f32[:])
-        zeros = keep.tile([P, BANK], BF16)
+        zeros = keep.tile([P, P], F32)
         nc.vector.memset(zeros[:], 0.0)
         ones = keep.tile([P, P], BF16)
         nc.vector.memset(ones[:], 1.0 / H_ROWS)
@@ -80,28 +80,58 @@ def tile_gateddynamicfusion_pa_kernel(tc, h_time, E_dyn, out):
         nc.scalar.activation(out=warm[:], in_=one[:], func=ACT.Sqrt)
 
         e_f32 = keep.tile([P, TILES, FEATS], F32)
-        grouped = keep.tile([P, TILES, PASSES, P, PACK], BF16, align_bytes=64)
+        grouped = keep.tile([P, PASSES, NODES, PACK], BF16, align_bytes=64)
         codes = keep.tile([P, PASSES, NODES], U32, align_bytes=64)
         scales = keep.tile([P, PASSES, NODES], U8, align_bytes=64)
         g_sb = keep.tile([P, TILES, NODES], F32)
 
+        first_sums = keep.tile([P, FEATS // BANK], F32)
         sumsq = keep.tile([P, TILES], F32)
         norm = keep.tile([P, TILES], F32)
         floored = keep.tile([P, TILES], F32)
         inv_norm = keep.tile([P, TILES], F32)
-        half_sums = keep.tile([P, TILES, HALVES], F32)
+        half_sums = keep.tile([P, HALVES, TILES], F32)
         doubled = keep.tile([P, TILES], F32)
-        denom = keep.tile([P, TILES], F32)
-        w_part = keep.tile([P, TILES], F32)
 
         psum = ctx.enter_context(tc.psum_pool(name="psum", bufs=1))
 
         def bank_tile(name, bank, shape):
             return psum.tile(shape, F32, name=name, offset=bank * BANK_BYTES)
 
+        sums = {}
+        FIRST = TILES // HALVES
+        order = [(i, 0) for i in range(FIRST)] + [(i, 1) for i in range(FIRST)]
+        for i in range(FIRST, TILES):
+            order += [(i, 0), (i, 1)]
+
+        def products(n, lo=0, hi=BANK):
+            i, b = order[n]
+            rows = slice(i * P, (i + 1) * P)
+            cols = slice(b * BANK + lo, b * BANK + hi)
+            if lo == 0:
+                sums[n] = bank_tile("acc%d" % n, RING_START + (TILES + n) % RING, [P, BANK])
+            for g in range(PASSES):
+                nc.tensor.matmul_mx(
+                    out=sums[n][:, lo:hi],
+                    lhsT=codes[:, g, rows].bitcast(FP8X4),
+                    lhsT_scale=scales[:, g, rows],
+                    rhs=codes[:, g, cols].bitcast(FP8X4),
+                    rhs_scale=scales[:, g, cols],
+                    start=(g == 0),
+                    stop=(g == PASSES - 1),
+                )
+
         with ExitStack():
+
+            def keep_warm(name, bank, count):
+                idle = bank_tile(name, bank, [P, P])
+                for n in range(count):
+                    nc.tensor.matmul(
+                        out=idle[:], lhsT=zeros[:], rhs=zeros[:], start=True, stop=True
+                    )
+
+            keep_warm("idle", PSUM_BANKS - 1, WARM_UPS)
             h_part = bank_tile("h_part", RING_START, [P, BLOCKS, len(COLUMN_SLICES), ONES])
-            idle = bank_tile("idle", RING_START + 1, [P, BANK])
             h_mean = [bank_tile("h_mean%d" % b, b, [P, BANK]) for b in range(FEATS // BANK)]
             h_sum = keep.tile([P, BLOCKS], F32)
 
@@ -136,10 +166,6 @@ def tile_gateddynamicfusion_pa_kernel(tc, h_time, E_dyn, out):
                         is_transpose=True,
                     )
 
-            for n in range(WARM_UPS):
-                nc.tensor.matmul(
-                    out=idle[:], lhsT=zeros[:, 0:P], rhs=zeros[:], start=True, stop=True
-                )
             for s in range(SLICES_BEFORE_JOIN):
                 if s in COLUMN_SLICES:
                     sum_slice(s)
@@ -158,13 +184,10 @@ def tile_gateddynamicfusion_pa_kernel(tc, h_time, E_dyn, out):
                     out=e_f32[:, t, cols], in0=e_sb[:, t, cols], in1=h_mean[b][:], op=ALU.add
                 )
 
-            def sum_squares(t):
+            def sum_squares(t, cols, total):
                 squares = work.tile([P, FEATS], BF16)
                 nc.scalar.activation(
-                    out=squares[:],
-                    in_=e_f32[:, t, :],
-                    func=ACT.Square,
-                    accum_out=sumsq[:, t : t + 1],
+                    out=squares[:, cols], in_=e_f32[:, t, cols], func=ACT.Square, accum_out=total
                 )
 
             def roots(tiles):
@@ -201,78 +224,73 @@ def tile_gateddynamicfusion_pa_kernel(tc, h_time, E_dyn, out):
                     for u in range(PAIRS):
                         nc.tensor.transpose(e_t[:, g, u, :], words[:, u, g, :], ident_f32[:])
                 flipped[t] = e_t
+                if t in WARM_AFTER:
+                    keep_warm("idle%d" % t, *WARM_AFTER[t])
 
             def regroup(t):
                 copy = nc.vector.tensor_copy if t in REGROUPED_BY_VECTOR else nc.scalar.copy
                 copy(
-                    out=grouped[:, t, :, :, :].bitcast(F32),
+                    out=grouped[:, :, t * P : (t + 1) * P, :].bitcast(F32),
                     in_=flipped[t][:].rearrange("p g u r -> p g r u"),
                 )
 
-            def quantise(t):
-                nodes = slice(t * P, (t + 1) * P)
+            def quantise(tiles):
+                nodes = slice(tiles.start * P, tiles.stop * P)
                 for g in range(PASSES):
                     nc.vector.quantize_mx(
                         out=codes[:, g, nodes].bitcast(FP8X4),
                         scales=scales[:, g, nodes],
-                        in_=grouped[:, t, g, :, :].rearrange("p r q -> p (r q)"),
+                        in_=grouped[:, g, nodes, :].rearrange("p r q -> p (r q)"),
                     )
 
             for t in range(TILES):
                 for b in range(FEATS // BANK):
                     add_mean(t, b)
+                    if t == 0:
+                        cols = slice(b * BANK, (b + 1) * BANK)
+                        sum_squares(t, cols, first_sums[:, b : b + 1])
+                if t == 1:
+                    nc.vector.tensor_tensor(
+                        out=sumsq[:, 0:1],
+                        in0=first_sums[:, 0:1],
+                        in1=first_sums[:, 1:2],
+                        op=ALU.add,
+                    )
                 for group in NORM_GROUPS:
                     if t == min(group.stop - 1 + INVERT_LAG, TILES - 1) and group.stop < TILES:
                         invert(group)
                         for u in range(group.start, group.stop):
                             scale_and_flip(u)
-                sum_squares(t)
+                if t > 0:
+                    sum_squares(t, slice(0, FEATS), sumsq[:, t : t + 1])
                 for group in NORM_GROUPS:
                     if t == group.stop - 1:
                         roots(group)
-            for t in range(2):
-                regroup(t)
-            for t in range(2):
-                quantise(t)
+            regroup(0)
+            regroup(1)
             invert(group)
-            for t in range(group.start, group.stop):
-                scale_and_flip(t)
-            for t in range(2, TILES):
+            quantise(slice(0, 2))
+            regroup(2)
+            regroup(3)
+            products(0, 0, 2 * P)
+            scale_and_flip(7)
+            scale_and_flip(6)
+            products(1, 0, 2 * P)
+            quantise(slice(2, 4))
+            for t in (4, 5, 7, 6):
                 regroup(t)
-            for t in range(2, TILES):
-                quantise(t)
+            quantise(slice(4, 6))
+            quantise(slice(7, 8))
+            quantise(slice(6, 7))
 
-        sums = {}
         w_free = [bank_tile("w_free%d" % b, b, [P, BANK]) for b in range(HALVES)]
-
-        FIRST = TILES // HALVES
-        order = [(i, 0) for i in range(FIRST)] + [(i, 1) for i in range(FIRST)]
-        for i in range(FIRST, TILES):
-            order += [(i, 0), (i, 1)]
-
-        def products(n):
-            i, b = order[n]
-            rows = slice(i * P, (i + 1) * P)
-            cols = slice(b * BANK, (b + 1) * BANK)
-            acc = bank_tile("acc%d" % n, RING_START + (TILES + n) % RING, [P, BANK])
-            for g in range(PASSES):
-                nc.tensor.matmul_mx(
-                    out=acc[:],
-                    lhsT=codes[:, g, rows].bitcast(FP8X4),
-                    lhsT_scale=scales[:, g, rows],
-                    rhs=codes[:, g, cols].bitcast(FP8X4),
-                    rhs_scale=scales[:, g, cols],
-                    start=(g == 0),
-                    stop=(g == PASSES - 1),
-                )
-            sums[n] = acc
 
         def finish(r, b, lo, hi):
             cols = slice(b * BANK + lo, b * BANK + hi)
             nc.vector.scalar_tensor_tensor(
                 out=g_sb[:, r, cols],
                 in0=w_free[b][:, lo:hi],
-                scalar=w_part[:, r : r + 1],
+                scalar=w_tiles[r],
                 in1=g_sb[:, r, cols],
                 op0=ALU.add,
                 op1=ALU.mult,
@@ -281,7 +299,7 @@ def tile_gateddynamicfusion_pa_kernel(tc, h_time, E_dyn, out):
         def relu(n):
             i, b = order[n]
             half = g_sb[:, i, b * BANK : (b + 1) * BANK]
-            half_sum = half_sums[:, i, b : b + 1]
+            half_sum = half_sums[:, b, i : i + 1]
             if (i, b) in RELU_BY_VECTOR:
                 nc.vector.tensor_scalar(
                     out=half,
@@ -294,77 +312,103 @@ def tile_gateddynamicfusion_pa_kernel(tc, h_time, E_dyn, out):
                 )
             else:
                 nc.scalar.activation(out=half, in_=sums[n][:], func=ACT.Relu, accum_out=half_sum)
-            if b == 0:
+
+        def double(tiles):
+            nc.gpsimd.tensor_scalar(
+                out=doubled[:, tiles],
+                in0=half_sums[:, 0, tiles],
+                scalar1=2.0,
+                scalar2=2.0 * ROWSUM_EPS,
+                op0=ALU.mult,
+                op1=ALU.add,
+            )
+
+        w_tiles = {}
+
+        def weigh(tiles):
+            count = tiles.stop - tiles.start
+            denom = keep.tile([P, count], F32, name="denom%d" % tiles.start)
+            w_part = keep.tile([P, count], F32, name="w_part%d" % tiles.start)
+            for i in range(tiles.start, tiles.stop):
+                w_tiles[i] = w_part[:, i - tiles.start : i - tiles.start + 1]
+            if FIRST < tiles.stop <= FIRST + 2:
                 nc.gpsimd.tensor_scalar(
-                    out=doubled[:, i : i + 1],
-                    in0=half_sums[:, i, 0:1],
+                    out=denom[:],
+                    in0=half_sums[:, 1, tiles],
                     scalar1=2.0,
-                    scalar2=2.0 * ROWSUM_EPS,
+                    scalar2=doubled[:, tiles],
                     op0=ALU.mult,
                     op1=ALU.add,
+                )
+                nc.gpsimd.tensor_tensor(
+                    out=w_part[:], in0=denom[:], in1=minus_one[:], op=ALU.pow
                 )
             else:
-                engine = nc.vector if i == TILES - 1 else nc.gpsimd
-                engine.tensor_scalar(
-                    out=denom[:, i : i + 1],
-                    in0=half_sums[:, i, 1:2],
-                    scalar1=2.0,
-                    scalar2=doubled[:, i : i + 1],
+                nc.vector.scalar_tensor_tensor(
+                    out=denom[:],
+                    in0=half_sums[:, 1, tiles],
+                    scalar=2.0,
+                    in1=doubled[:, tiles],
                     op0=ALU.mult,
                     op1=ALU.add,
                 )
-                if i == TILES - 1:
-                    nc.vector.reciprocal(out=w_part[:, i : i + 1], in_=denom[:, i : i + 1])
-                else:
-                    nc.gpsimd.tensor_tensor(
-                        out=w_part[:, i : i + 1],
-                        in0=denom[:, i : i + 1],
-                        in1=minus_one[:],
-                        op=ALU.pow,
-                    )
+                nc.vector.reciprocal(out=w_part[:], in_=denom[:])
 
-        def complete(i):
-            bank, lo = divmod(i * P, BANK)
-            nc.tensor.transpose(
-                w_free[bank][:, lo : lo + P],
-                w_part[:, i : i + 1].to_broadcast([P, P]),
-                ident_f32[:],
-            )
-            for b in range(bank):
-                finish(i, b, 0, BANK)
-                full = slice(b * BANK, (b + 1) * BANK)
-                nc.sync.dma_start(out=out_rows[:, i, full], in_=g_sb[:, i, full])
-            if i > 0 and i not in MIRRORED:
-                for r in range(i):
-                    finish(r, bank, lo, lo + P)
-                above = slice(i * P, (i + 1) * P)
-                nc.sync.dma_start(out=out_rows[:, 0:i, above], in_=g_sb[:, 0:i, above])
-            finish(i, bank, 0, lo + P)
-            rest = slice(bank * BANK, (i + 1) * P)
-            nc.sync.dma_start(out=out_rows[:, i, rest], in_=g_sb[:, i, rest])
+        def spread(tiles):
+            for i in range(tiles.start, tiles.stop):
+                bank, lo = divmod(i * P, BANK)
+                nc.tensor.transpose(
+                    w_free[bank][:, lo : lo + P],
+                    w_tiles[i].to_broadcast([P, P]),
+                    ident_f32[:],
+                )
+
+        def store(rows, cols):
+            nc.sync.dma_start(out=out_rows[:, rows, cols], in_=g_sb[:, rows, cols])
 
         def mirror(i):
-            above = slice(i * P, (i + 1) * P)
-            for r in range(0, i, BANK // P):
-                tiles = slice(r, min(r + BANK // P, i))
-                count = tiles.stop - tiles.start
-                m_t = bank_tile("m_t%d_%d" % (i, r), RING_START + (i * HALVES + r // 4) % RING, [P, BANK // P, P])
-                for q in range(count):
-                    nc.tensor.transpose(
-                        m_t[:, q, :], g_sb[:, i, (r + q) * P : (r + q + 1) * P], ident_f32[:]
-                    )
-                nc.scalar.copy(out=g_sb[:, tiles, above], in_=m_t[:, 0:count, :])
-                nc.sync.dma_start(out=out_rows[:, tiles, above], in_=g_sb[:, tiles, above])
+            m_t = bank_tile("m_t%d" % i, RING_START + i - FIRST, [P, FIRST, P])
+            for r in range(FIRST):
+                nc.tensor.transpose(m_t[:, r, :], g_sb[:, i, r * P : (r + 1) * P], ident_f32[:])
+            mirrors[i] = m_t
 
+        def copy_mirror(i):
+            nc.scalar.copy(out=g_sb[:, 0:FIRST, i * P : (i + 1) * P], in_=mirrors[i][:])
+
+        mirrors = {}
         units = len(order)
         for n in range(AHEAD):
-            products(n)
+            products(n, 2 * P)
         for n in range(units):
             relu(n)
             if n + AHEAD < units:
                 products(n + AHEAD)
-            if n > 0 and order[n - 1][1] == HALVES - 1:
-                complete(order[n - 1][0])
-        complete(TILES - 1)
-        for i in MIRRORED:
-            mirror(i)
+            i, b = order[n]
+            tiles = slice(i, i + 1) if i >= FIRST else slice(0, FIRST)
+            if tiles.stop - 1 == i:
+                if b == 0:
+                    double(tiles)
+                else:
+                    weigh(tiles)
+                    if i < FIRST:
+                        spread(tiles)
+                    for r in range(tiles.start, tiles.stop):
+                        finish(r, 0, 0, BANK)
+                        store(r, slice(0, BANK))
+            if n == units - 2:
+                spread(slice(4, 6))
+                mirror(4)
+        mirror(5)
+        spread(slice(6, 8))
+        copy_mirror(4)
+        copy_mirror(5)
+        store(slice(0, FIRST), slice(4 * P, 6 * P))
+        mirror(6)
+        mirror(7)
+        copy_mirror(6)
+        copy_mirror(7)
+        for r in range(FIRST, TILES):
+            finish(r, 1, 0, BANK)
+            if r == 4:
+                store(slice(0, FIRST), slice(6 * P, 8 * P))
+            store(r, slice(BANK, NODES))

@@ -36,8 +36,7 @@ NORM_FLOOR = 1e-12
 ROWSUM_EPS = 1e-6
 SQRT_GUARD = 2.0 ** -110
 
-NORM_GROUPS = (slice(0, 2), slice(2, 4), slice(4, 6), slice(6, 8))
-INVERT_LAG = 2
+INVERTED_AFTER = {(3, 0): slice(0, 2), (5, 1): slice(2, 4), (7, 1): slice(4, 6)}
 SCALED_BY_VECTOR = (4, 7)
 REGROUPED_BY_VECTOR = (0, 1)
 RELU_BY_VECTOR = ((3, 0), (0, 1), (1, 1))
@@ -80,7 +79,10 @@ def tile_gateddynamicfusion_pa_kernel(tc, h_time, E_dyn, out):
         nc.scalar.activation(out=warm[:], in_=one[:], func=ACT.Sqrt)
 
         e_f32 = keep.tile([P, TILES, FEATS], F32)
-        grouped = keep.tile([P, PASSES, NODES, PACK], BF16, align_bytes=64)
+        grouped = [
+            keep.tile([P, PASSES, P, PACK], BF16, name="grouped%d" % t, align_bytes=64)
+            for t in range(TILES)
+        ]
         codes = keep.tile([P, PASSES, NODES], U32, align_bytes=64)
         scales = keep.tile([P, PASSES, NODES], U8, align_bytes=64)
         g_sb = keep.tile([P, TILES, NODES], F32)
@@ -230,17 +232,17 @@ def tile_gateddynamicfusion_pa_kernel(tc, h_time, E_dyn, out):
             def regroup(t):
                 copy = nc.vector.tensor_copy if t in REGROUPED_BY_VECTOR else nc.scalar.copy
                 copy(
-                    out=grouped[:, :, t * P : (t + 1) * P, :].bitcast(F32),
+                    out=grouped[t][:].bitcast(F32),
                     in_=flipped[t][:].rearrange("p g u r -> p g r u"),
                 )
 
-            def quantise(tiles):
-                nodes = slice(tiles.start * P, tiles.stop * P)
+            def quantise(t):
+                nodes = slice(t * P, (t + 1) * P)
                 for g in range(PASSES):
                     nc.vector.quantize_mx(
                         out=codes[:, g, nodes].bitcast(FP8X4),
                         scales=scales[:, g, nodes],
-                        in_=grouped[:, g, nodes, :].rearrange("p r q -> p (r q)"),
+                        in_=grouped[t][:, g, :, :].rearrange("p r q -> p (r q)"),
                     )
 
             for t in range(TILES):
@@ -249,6 +251,11 @@ def tile_gateddynamicfusion_pa_kernel(tc, h_time, E_dyn, out):
                     if t == 0:
                         cols = slice(b * BANK, (b + 1) * BANK)
                         sum_squares(t, cols, first_sums[:, b : b + 1])
+                    if (t, b) in INVERTED_AFTER:
+                        group = INVERTED_AFTER[t, b]
+                        invert(group)
+                        for u in range(group.start, group.stop):
+                            scale_and_flip(u)
                 if t == 1:
                     nc.vector.tensor_tensor(
                         out=sumsq[:, 0:1],
@@ -256,32 +263,27 @@ def tile_gateddynamicfusion_pa_kernel(tc, h_time, E_dyn, out):
                         in1=first_sums[:, 1:2],
                         op=ALU.add,
                     )
-                for group in NORM_GROUPS:
-                    if t == min(group.stop - 1 + INVERT_LAG, TILES - 1) and group.stop < TILES:
-                        invert(group)
-                        for u in range(group.start, group.stop):
-                            scale_and_flip(u)
                 if t > 0:
                     sum_squares(t, slice(0, FEATS), sumsq[:, t : t + 1])
-                for group in NORM_GROUPS:
-                    if t == group.stop - 1:
-                        roots(group)
+                if t % 2 == 1:
+                    roots(slice(t - 1, t + 1))
             regroup(0)
             regroup(1)
-            invert(group)
-            quantise(slice(0, 2))
+            invert(slice(6, 8))
+            quantise(0)
+            quantise(1)
             regroup(2)
             regroup(3)
             products(0, 0, 2 * P)
             scale_and_flip(7)
             scale_and_flip(6)
             products(1, 0, 2 * P)
-            quantise(slice(2, 4))
+            quantise(2)
+            quantise(3)
             for t in (4, 5, 7, 6):
                 regroup(t)
-            quantise(slice(4, 6))
-            quantise(slice(7, 8))
-            quantise(slice(6, 7))
+            for t in (4, 5, 7, 6):
+                quantise(t)
 
         w_free = [bank_tile("w_free%d" % b, b, [P, BANK]) for b in range(HALVES)]
 
@@ -298,7 +300,11 @@ def tile_gateddynamicfusion_pa_kernel(tc, h_time, E_dyn, out):
 
         def relu(n):
             i, b = order[n]
-            half = g_sb[:, i, b * BANK : (b + 1) * BANK]
+            if b == 1 and i < FIRST:
+                unused = work.tile([P, BANK], BF16)
+                half = unused[:]
+            else:
+                half = g_sb[:, i, b * BANK : (b + 1) * BANK]
             half_sum = half_sums[:, b, i : i + 1]
             if (i, b) in RELU_BY_VECTOR:
                 nc.vector.tensor_scalar(
@@ -373,7 +379,18 @@ def tile_gateddynamicfusion_pa_kernel(tc, h_time, E_dyn, out):
             mirrors[i] = m_t
 
         def copy_mirror(i):
-            nc.scalar.copy(out=g_sb[:, 0:FIRST, i * P : (i + 1) * P], in_=mirrors[i][:])
+            nc.scalar.copy(out=upper[i // 2][:, :, i % 2, :], in_=mirrors[i][:])
+
+        def store_mirrors(i):
+            nc.sync.dma_start(
+                out=out_rows[:, 0:FIRST, i * P : (i + 2) * P],
+                in_=upper[i // 2][:].rearrange("p r i c -> p r (i c)"),
+            )
+
+        upper = {
+            j: keep.tile([P, FIRST, 2, P], F32, name="upper%d" % j)
+            for j in range(FIRST // 2, TILES // 2)
+        }
 
         mirrors = {}
         units = len(order)
@@ -402,7 +419,7 @@ def tile_gateddynamicfusion_pa_kernel(tc, h_time, E_dyn, out):
         spread(slice(6, 8))
         copy_mirror(4)
         copy_mirror(5)
-        store(slice(0, FIRST), slice(4 * P, 6 * P))
+        store_mirrors(4)
         mirror(6)
         mirror(7)
         copy_mirror(6)
@@ -410,5 +427,5 @@ def tile_gateddynamicfusion_pa_kernel(tc, h_time, E_dyn, out):
         for r in range(FIRST, TILES):
             finish(r, 1, 0, BANK)
             if r == 4:
-                store(slice(0, FIRST), slice(6 * P, 8 * P))
+                store_mirrors(6)
             store(r, slice(BANK, NODES))

@@ -37,7 +37,8 @@ ROWSUM_EPS = 1e-6
 SQRT_GUARD = 2.0 ** -110
 
 INVERTED_AFTER = {(3, 0): slice(0, 2), (5, 1): slice(2, 4), (7, 1): slice(4, 6)}
-SCALED_BY_VECTOR = (4, 7)
+INVERTED_BY_GPSIMD = (2,)
+SCALED_BY_VECTOR = (4, 5, 6, 7)
 REGROUPED_BY_VECTOR = (0, 1)
 RELU_BY_VECTOR = ((3, 0), (0, 1), (1, 1))
 AHEAD = 2
@@ -73,8 +74,10 @@ def tile_gateddynamicfusion_pa_kernel(tc, h_time, E_dyn, out):
         nc.vector.memset(ones[:], 1.0 / H_ROWS)
         one = keep.tile([P, 1], F32)
         nc.vector.memset(one[:], 1.0)
-        minus_one = keep.tile([P, 1], F32)
-        nc.vector.memset(minus_one[:], -1.0)
+        minus_ones = keep.tile([P, 2], F32)
+        nc.vector.memset(minus_ones[:], -1.0)
+        gp_floored = keep.tile([P, 2], F32)
+        gp_inv_norm = keep.tile([P, 2], F32)
         warm = keep.tile([P, 1], F32)
         nc.scalar.activation(out=warm[:], in_=one[:], func=ACT.Sqrt)
 
@@ -197,7 +200,25 @@ def tile_gateddynamicfusion_pa_kernel(tc, h_time, E_dyn, out):
                     out=norm[:, tiles], in_=sumsq[:, tiles], func=ACT.Sqrt, bias=SQRT_GUARD
                 )
 
+            inv_norms = {}
+
             def invert(tiles):
+                if tiles.start in INVERTED_BY_GPSIMD:
+                    nc.gpsimd.tensor_scalar(
+                        out=gp_floored[:],
+                        in0=norm[:, tiles],
+                        scalar1=NORM_FLOOR,
+                        scalar2=None,
+                        op0=ALU.max,
+                    )
+                    nc.gpsimd.tensor_tensor(
+                        out=gp_inv_norm[:], in0=gp_floored[:], in1=minus_ones[:], op=ALU.pow
+                    )
+                    for t in range(tiles.start, tiles.stop):
+                        inv_norms[t] = gp_inv_norm[:, t - tiles.start : t - tiles.start + 1]
+                    return
+                for t in range(tiles.start, tiles.stop):
+                    inv_norms[t] = inv_norm[:, t : t + 1]
                 nc.vector.tensor_scalar(
                     out=floored[:, tiles],
                     in0=norm[:, tiles],
@@ -215,7 +236,7 @@ def tile_gateddynamicfusion_pa_kernel(tc, h_time, E_dyn, out):
                 engine.tensor_scalar(
                     out=e_cur[:].rearrange("p (u w e) -> p u w e", u=PAIRS, e=2),
                     in0=e_f32[:, t, :].rearrange("p (w u e) -> p u w e", u=PAIRS, e=2),
-                    scalar1=inv_norm[:, t : t + 1],
+                    scalar1=inv_norms[t],
                     scalar2=0.0,
                     op0=ALU.mult,
                     op1=ALU.add,
@@ -270,19 +291,19 @@ def tile_gateddynamicfusion_pa_kernel(tc, h_time, E_dyn, out):
             regroup(0)
             regroup(1)
             invert(slice(6, 8))
-            quantise(0)
-            quantise(1)
             regroup(2)
             regroup(3)
-            products(0, 0, 2 * P)
-            scale_and_flip(7)
             scale_and_flip(6)
+            scale_and_flip(7)
+            quantise(0)
+            quantise(1)
+            products(0, 0, 2 * P)
             products(1, 0, 2 * P)
             quantise(2)
             quantise(3)
-            for t in (4, 5, 7, 6):
+            for t in range(4, TILES):
                 regroup(t)
-            for t in (4, 5, 7, 6):
+            for t in range(4, TILES):
                 quantise(t)
 
         w_free = [bank_tile("w_free%d" % b, b, [P, BANK]) for b in range(HALVES)]
@@ -347,7 +368,7 @@ def tile_gateddynamicfusion_pa_kernel(tc, h_time, E_dyn, out):
                     op1=ALU.add,
                 )
                 nc.gpsimd.tensor_tensor(
-                    out=w_part[:], in0=denom[:], in1=minus_one[:], op=ALU.pow
+                    out=w_part[:], in0=denom[:], in1=minus_ones[:, 0:1], op=ALU.pow
                 )
             else:
                 nc.vector.scalar_tensor_tensor(

@@ -28,6 +28,7 @@ BANK_BYTES = 4 * BANK
 HALVES = NODES // BANK
 RING_START = HALVES
 RING = PSUM_BANKS - RING_START
+H_LOADS = (slice(0, 2), slice(2, 4), slice(4, 6), slice(6, 7), slice(7, 8))
 ONES = 2
 COLUMN_SLICES = (1, 2, 4, 5)
 SLICES_BEFORE_JOIN = 7
@@ -36,7 +37,7 @@ NORM_FLOOR = 1e-12
 ROWSUM_EPS = 1e-6
 SQRT_GUARD = 2.0 ** -110
 
-INVERTED_AFTER = {(3, 0): slice(0, 2), (5, 1): slice(2, 4), (7, 1): slice(4, 6)}
+INVERTED_AFTER = {(3, 0): slice(0, 2), (5, 1): slice(2, 4)}
 INVERTED_BY_GPSIMD = (2,)
 SCALED_BY_VECTOR = (4, 5, 6, 7)
 REGROUPED_BY_VECTOR = (0, 1)
@@ -61,7 +62,7 @@ def tile_gateddynamicfusion_pa_kernel(tc, h_time, E_dyn, out):
 
         h_sb = keep.tile([P, SLICES, FEATS], BF16)
         e_sb = keep.tile([P, TILES, FEATS], BF16)
-        for s in range(SLICES):
+        for s in H_LOADS:
             nc.sync.dma_start(out=h_sb[:, s, :], in_=h_rows[:, s, :])
         for t in range(TILES):
             nc.sync.dma_start(out=e_sb[:, t, :], in_=e_rows[:, t, :])
@@ -290,6 +291,9 @@ def tile_gateddynamicfusion_pa_kernel(tc, h_time, E_dyn, out):
                     roots(slice(t - 1, t + 1))
             regroup(0)
             regroup(1)
+            invert(slice(4, 6))
+            scale_and_flip(4)
+            scale_and_flip(5)
             invert(slice(6, 8))
             regroup(2)
             regroup(3)

@@ -37,11 +37,10 @@ NORM_FLOOR = 1e-12
 ROWSUM_EPS = 1e-6
 SQRT_GUARD = 2.0 ** -110
 
-INVERTED_AFTER = {(3, 0): slice(0, 2), (5, 1): slice(2, 4)}
-INVERTED_BY_GPSIMD = (2,)
+INVERTED_BY_GPSIMD = {0: slice(0, 1), 1: slice(1, 2), 3: slice(2, 4)}
 SCALED_BY_VECTOR = (4, 5, 6, 7)
 REGROUPED_BY_VECTOR = (0, 1)
-RELU_BY_VECTOR = ((3, 0), (0, 1), (1, 1))
+RELU_BY_VECTOR = ((0, 1), (1, 1))
 AHEAD = 2
 WARM_UPS = 4
 WARM_AFTER = {1: (7, 2), 2: (7, 2), 4: (1, 1), 5: (1, 1)}
@@ -77,8 +76,8 @@ def tile_gateddynamicfusion_pa_kernel(tc, h_time, E_dyn, out):
         nc.vector.memset(one[:], 1.0)
         minus_ones = keep.tile([P, 2], F32)
         nc.vector.memset(minus_ones[:], -1.0)
-        gp_floored = keep.tile([P, 2], F32)
-        gp_inv_norm = keep.tile([P, 2], F32)
+        minus_halves = keep.tile([P, 2], F32)
+        nc.vector.memset(minus_halves[:], -0.5)
         warm = keep.tile([P, 1], F32)
         nc.scalar.activation(out=warm[:], in_=one[:], func=ACT.Sqrt)
 
@@ -196,30 +195,41 @@ def tile_gateddynamicfusion_pa_kernel(tc, h_time, E_dyn, out):
                     out=squares[:, cols], in_=e_f32[:, t, cols], func=ACT.Square, accum_out=total
                 )
 
+            inv_norms = {}
+
+            def invert_by_gpsimd(tiles):
+                count = tiles.stop - tiles.start
+                floored_sums = keep.tile([P, count], F32, name="floored_sums%d" % tiles.start)
+                powers = keep.tile([P, count], F32, name="powers%d" % tiles.start)
+                if tiles.start == 0:
+                    nc.gpsimd.tensor_scalar(
+                        out=floored_sums[:],
+                        in0=first_sums[:, 0:1],
+                        scalar1=first_sums[:, 1:2],
+                        scalar2=NORM_FLOOR * NORM_FLOOR,
+                        op0=ALU.add,
+                        op1=ALU.max,
+                    )
+                else:
+                    nc.gpsimd.tensor_scalar(
+                        out=floored_sums[:],
+                        in0=sumsq[:, tiles],
+                        scalar1=NORM_FLOOR * NORM_FLOOR,
+                        scalar2=None,
+                        op0=ALU.max,
+                    )
+                nc.gpsimd.tensor_tensor(
+                    out=powers[:], in0=floored_sums[:], in1=minus_halves[:, 0:count], op=ALU.pow
+                )
+                for t in range(tiles.start, tiles.stop):
+                    inv_norms[t] = powers[:, t - tiles.start : t - tiles.start + 1]
+
             def roots(tiles):
                 nc.scalar.activation(
                     out=norm[:, tiles], in_=sumsq[:, tiles], func=ACT.Sqrt, bias=SQRT_GUARD
                 )
 
-            inv_norms = {}
-
             def invert(tiles):
-                if tiles.start in INVERTED_BY_GPSIMD:
-                    nc.gpsimd.tensor_scalar(
-                        out=gp_floored[:],
-                        in0=norm[:, tiles],
-                        scalar1=NORM_FLOOR,
-                        scalar2=None,
-                        op0=ALU.max,
-                    )
-                    nc.gpsimd.tensor_tensor(
-                        out=gp_inv_norm[:], in0=gp_floored[:], in1=minus_ones[:], op=ALU.pow
-                    )
-                    for t in range(tiles.start, tiles.stop):
-                        inv_norms[t] = gp_inv_norm[:, t - tiles.start : t - tiles.start + 1]
-                    return
-                for t in range(tiles.start, tiles.stop):
-                    inv_norms[t] = inv_norm[:, t : t + 1]
                 nc.vector.tensor_scalar(
                     out=floored[:, tiles],
                     in0=norm[:, tiles],
@@ -228,6 +238,8 @@ def tile_gateddynamicfusion_pa_kernel(tc, h_time, E_dyn, out):
                     op0=ALU.max,
                 )
                 nc.vector.reciprocal(out=inv_norm[:, tiles], in_=floored[:, tiles])
+                for t in range(tiles.start, tiles.stop):
+                    inv_norms[t] = inv_norm[:, t : t + 1]
 
             flipped = {}
 
@@ -273,22 +285,15 @@ def tile_gateddynamicfusion_pa_kernel(tc, h_time, E_dyn, out):
                     if t == 0:
                         cols = slice(b * BANK, (b + 1) * BANK)
                         sum_squares(t, cols, first_sums[:, b : b + 1])
-                    if (t, b) in INVERTED_AFTER:
-                        group = INVERTED_AFTER[t, b]
-                        invert(group)
-                        for u in range(group.start, group.stop):
-                            scale_and_flip(u)
-                if t == 1:
-                    nc.vector.tensor_tensor(
-                        out=sumsq[:, 0:1],
-                        in0=first_sums[:, 0:1],
-                        in1=first_sums[:, 1:2],
-                        op=ALU.add,
-                    )
                 if t > 0:
                     sum_squares(t, slice(0, FEATS), sumsq[:, t : t + 1])
-                if t % 2 == 1:
+                if t in (5, 7):
                     roots(slice(t - 1, t + 1))
+                if t in INVERTED_BY_GPSIMD:
+                    tiles = INVERTED_BY_GPSIMD[t]
+                    invert_by_gpsimd(tiles)
+                    for u in range(tiles.start, tiles.stop):
+                        scale_and_flip(u)
             regroup(0)
             regroup(1)
             invert(slice(4, 6))
@@ -419,29 +424,37 @@ def tile_gateddynamicfusion_pa_kernel(tc, h_time, E_dyn, out):
 
         mirrors = {}
         units = len(order)
+        groups = [slice(0, 2), slice(2, 4)] + [slice(i, i + 1) for i in range(FIRST, TILES)]
         for n in range(AHEAD):
             products(n, 2 * P)
         for n in range(units):
             relu(n)
             if n + AHEAD < units:
                 products(n + AHEAD)
-            i, b = order[n]
-            tiles = slice(i, i + 1) if i >= FIRST else slice(0, FIRST)
-            if tiles.stop - 1 == i:
-                if b == 0:
+            for tiles in groups:
+                if (tiles.stop - 1, 0) == order[n]:
                     double(tiles)
-                else:
+                if (tiles.stop - 1, 1) == order[n]:
                     weigh(tiles)
-                    if i < FIRST:
-                        spread(tiles)
-                    for r in range(tiles.start, tiles.stop):
-                        finish(r, 0, 0, BANK)
-                        store(r, slice(0, BANK))
-            if n == units - 2:
-                spread(slice(4, 6))
-                mirror(4)
+            if n == 5 + 1:
+                spread(slice(0, 2))
+                for r in (0, 1):
+                    finish(r, 0, 0, 2 * P)
+                    store(r, slice(0, 2 * P))
+            if n == 7 + 1:
+                spread(slice(2, 4))
+                for r in (0, 1):
+                    finish(r, 0, 2 * P, BANK)
+                    store(r, slice(2 * P, BANK))
+                for r in (2, 3):
+                    finish(r, 0, 0, BANK)
+                    store(r, slice(0, BANK))
+            if order[n][0] >= FIRST and order[n][1] == 1:
+                finish(order[n][0], 0, 0, BANK)
+                store(order[n][0], slice(0, BANK))
+        mirror(4)
         mirror(5)
-        spread(slice(6, 8))
+        spread(slice(4, 8))
         copy_mirror(4)
         copy_mirror(5)
         store_mirrors(4)

@@ -37,9 +37,9 @@ NORM_FLOOR = 1e-12
 ROWSUM_EPS = 1e-6
 SQRT_GUARD = 2.0 ** -110
 
-INVERTED_BY_GPSIMD = {0: slice(0, 1), 1: slice(1, 2), 3: slice(2, 4)}
-SCALED_BY_VECTOR = (4, 5, 6, 7)
-REGROUPED_BY_VECTOR = (0, 1)
+INVERTED_BY_GPSIMD = {0: slice(0, 1), 1: slice(1, 2), 2: slice(2, 3)}
+SCALED_BY_VECTOR = (3, 4, 5, 6, 7)
+REGROUPED_BY_VECTOR = (0,)
 RELU_BY_VECTOR = ((0, 1), (1, 1))
 AHEAD = 2
 WARM_UPS = 4
@@ -287,8 +287,10 @@ def tile_gateddynamicfusion_pa_kernel(tc, h_time, E_dyn, out):
                         sum_squares(t, cols, first_sums[:, b : b + 1])
                 if t > 0:
                     sum_squares(t, slice(0, FEATS), sumsq[:, t : t + 1])
-                if t in (5, 7):
-                    roots(slice(t - 1, t + 1))
+                if t == 5:
+                    roots(slice(3, 6))
+                if t == 7:
+                    roots(slice(6, 8))
                 if t in INVERTED_BY_GPSIMD:
                     tiles = INVERTED_BY_GPSIMD[t]
                     invert_by_gpsimd(tiles)
@@ -296,7 +298,8 @@ def tile_gateddynamicfusion_pa_kernel(tc, h_time, E_dyn, out):
                         scale_and_flip(u)
             regroup(0)
             regroup(1)
-            invert(slice(4, 6))
+            invert(slice(3, 6))
+            scale_and_flip(3)
             scale_and_flip(4)
             scale_and_flip(5)
             invert(slice(6, 8))

@@ -39,7 +39,7 @@ SQRT_GUARD = 2.0 ** -110
 
 INVERTED_BY_GPSIMD = {0: slice(0, 1), 1: slice(1, 2), 2: slice(2, 3)}
 SCALED_BY_VECTOR = (3, 4, 5, 6, 7)
-REGROUPED_BY_VECTOR = (0,)
+REGROUPED_BY_VECTOR = ()
 RELU_BY_VECTOR = ((0, 1), (1, 1))
 AHEAD = 2
 WARM_UPS = 4

@@ -415,7 +415,7 @@ def tile_gateddynamicfusion_pa_kernel(tc, h_time, E_dyn, out):
             nc.scalar.copy(out=upper[i // 2][:, :, i % 2, :], in_=mirrors[i][:])
 
         def store_mirrors(i):
-            nc.sync.dma_start(
+            nc.scalar.dma_start(
                 out=out_rows[:, 0:FIRST, i * P : (i + 2) * P],
                 in_=upper[i // 2][:].rearrange("p r i c -> p r (i c)"),
             )
@@ -455,9 +455,14 @@ def tile_gateddynamicfusion_pa_kernel(tc, h_time, E_dyn, out):
             if order[n][0] >= FIRST and order[n][1] == 1:
                 finish(order[n][0], 0, 0, BANK)
                 store(order[n][0], slice(0, BANK))
+            if n == 13:
+                spread(slice(4, 6))
+                for r in (4, 5):
+                    finish(r, 1, 0, 2 * P)
+                    store(r, slice(BANK, BANK + 2 * P))
         mirror(4)
         mirror(5)
-        spread(slice(4, 8))
+        spread(slice(6, 8))
         copy_mirror(4)
         copy_mirror(5)
         store_mirrors(4)
@@ -465,8 +470,7 @@ def tile_gateddynamicfusion_pa_kernel(tc, h_time, E_dyn, out):
         mirror(7)
         copy_mirror(6)
         copy_mirror(7)
-        for r in range(FIRST, TILES):
-            finish(r, 1, 0, BANK)
-            if r == 4:
-                store_mirrors(6)
-            store(r, slice(BANK, NODES))
+        store_mirrors(6)
+        for r in (6, 7, 4, 5):
+            finish(r, 1, 2 * P if r < 6 else 0, BANK)
+            store(r, slice(BANK + (2 * P if r < 6 else 0), NODES))

from contextlib import ExitStack

import concourse.mybir as mybir
from concourse.masks import make_identity

F32 = mybir.dt.float32
BF16 = mybir.dt.bfloat16
U32 = mybir.dt.uint32
U8 = mybir.dt.uint8
FP8X4 = mybir.dt.float8_e4m3fn_x4
ALU = mybir.AluOpType
ACT = mybir.ActivationFunctionType
AXIS = mybir.AxisListType

P = 128
NODES = 1024
FEATS = 1024
H_ROWS = 1024
TILES = NODES // P
SLICES = H_ROWS // P
BLOCKS = FEATS // P
PACK = 4
PAIRS = PACK // 2
PASSES = FEATS // (P * PACK)
BANK = 512
PSUM_BANKS = 8
BANK_BYTES = 4 * BANK
HALVES = NODES // BANK
RING_START = HALVES
RING = PSUM_BANKS - RING_START
H_LOADS = (slice(0, 2), slice(2, 4), slice(4, 6), slice(6, 7), slice(7, 8))
ONES = 2
COLUMN_SLICES = (1, 2, 4, 5)
SLICES_BEFORE_JOIN = 7

NORM_FLOOR = 1e-12
ROWSUM_EPS = 1e-6
SQRT_GUARD = 2.0 ** -110

INVERTED_BY_GPSIMD = {0: slice(0, 1), 1: slice(1, 2), 2: slice(2, 3)}
SCALED_BY_VECTOR = (3, 4, 5, 6, 7)
REGROUPED_BY_VECTOR = ()
RELU_BY_VECTOR = ((0, 1), (1, 1))
AHEAD = 2
WARM_UPS = 4
WARM_AFTER = {1: (7, 2), 2: (7, 2), 4: (1, 1), 5: (1, 1)}

FLOPS = 2 * NODES * NODES * FEATS


def tile_gateddynamicfusion_pa_kernel(tc, h_time, E_dyn, out):
    nc = tc.nc
    h_rows = h_time.flatten_outer_dims().rearrange("(p s) k -> p s k", s=SLICES)
    e_rows = E_dyn.rearrange("(t p) k -> p t k", p=P)
    out_rows = out.rearrange("(t p) j -> p t j", p=P)

    with ExitStack() as ctx:
        ctx.enter_context(tc.manual_schedule())
        keep = ctx.enter_context(tc.tile_pool(name="keep", bufs=1))
        work = ctx.enter_context(tc.tile_pool(name="work", bufs=3))

        h_sb = keep.tile([P, SLICES, FEATS], BF16)
        e_sb = keep.tile([P, TILES, FEATS], BF16)
        for s in H_LOADS:
            nc.sync.dma_start(out=h_sb[:, s, :], in_=h_rows[:, s, :])
        for t in range(TILES):
            nc.sync.dma_start(out=e_sb[:, t, :], in_=e_rows[:, t, :])

        ident_f32 = keep.tile([P, P], F32)
        make_identity(nc, ident_f32[:])
        zeros = keep.tile([P, P], F32)
        nc.vector.memset(zeros[:], 0.0)
        ones = keep.tile([P, P], BF16)
        nc.vector.memset(ones[:], 1.0 / H_ROWS)
        one = keep.tile([P, 1], F32)
        nc.vector.memset(one[:], 1.0)
        minus_ones = keep.tile([P, 2], F32)
        nc.vector.memset(minus_ones[:], -1.0)
        minus_halves = keep.tile([P, 2], F32)
        nc.vector.memset(minus_halves[:], -0.5)
        warm = keep.tile([P, 1], F32)
        nc.scalar.activation(out=warm[:], in_=one[:], func=ACT.Sqrt)

        e_f32 = keep.tile([P, TILES, FEATS], F32)
        grouped = [
            keep.tile([P, PASSES, P, PACK], BF16, name="grouped%d" % t, align_bytes=64)
            for t in range(TILES)
        ]
        codes = keep.tile([P, PASSES, NODES], U32, align_bytes=64)
        scales = keep.tile([P, PASSES, NODES], U8, align_bytes=64)
        g_sb = keep.tile([P, TILES, NODES], F32)

        first_sums = keep.tile([P, FEATS // BANK], F32)
        sumsq = keep.tile([P, TILES], F32)
        norm = keep.tile([P, TILES], F32)
        floored = keep.tile([P, TILES], F32)
        inv_norm = keep.tile([P, TILES], F32)
        half_sums = keep.tile([P, HALVES, TILES], F32)
        doubled = keep.tile([P, TILES], F32)

        psum = ctx.enter_context(tc.psum_pool(name="psum", bufs=1))

        def bank_tile(name, bank, shape):
            return psum.tile(shape, F32, name=name, offset=bank * BANK_BYTES)

        sums = {}
        FIRST = TILES // HALVES
        order = [(i, 0) for i in range(FIRST)] + [(i, 1) for i in range(FIRST)]
        for i in range(FIRST, TILES):
            order += [(i, 0), (i, 1)]

        def products(n, lo=0, hi=BANK):
            i, b = order[n]
            rows = slice(i * P, (i + 1) * P)
            cols = slice(b * BANK + lo, b * BANK + hi)
            if lo == 0:
                sums[n] = bank_tile("acc%d" % n, RING_START + (TILES + n) % RING, [P, BANK])
            for g in range(PASSES):
                nc.tensor.matmul_mx(
                    out=sums[n][:, lo:hi],
                    lhsT=codes[:, g, rows].bitcast(FP8X4),
                    lhsT_scale=scales[:, g, rows],
                    rhs=codes[:, g, cols].bitcast(FP8X4),
                    rhs_scale=scales[:, g, cols],
                    start=(g == 0),
                    stop=(g == PASSES - 1),
                )

        with ExitStack():

            def keep_warm(name, bank, count):
                idle = bank_tile(name, bank, [P, P])
                for n in range(count):
                    nc.tensor.matmul(
                        out=idle[:], lhsT=zeros[:], rhs=zeros[:], start=True, stop=True
                    )

            keep_warm("idle", PSUM_BANKS - 1, WARM_UPS)
            h_part = bank_tile("h_part", RING_START, [P, BLOCKS, len(COLUMN_SLICES), ONES])
            h_mean = [bank_tile("h_mean%d" % b, b, [P, BANK]) for b in range(FEATS // BANK)]
            h_sum = keep.tile([P, BLOCKS], F32)

            def spread_slice(s, b):
                nc.tensor.matmul(
                    out=h_mean[b][:],
                    lhsT=ones[:],
                    rhs=h_sb[:, s, b * BANK : (b + 1) * BANK],
                    start=(s == 0),
                    stop=(s == SLICES - 1),
                )

            def sum_slice(s):
                for j in range(BLOCKS):
                    nc.tensor.matmul(
                        out=h_part[:, j, COLUMN_SLICES.index(s), :],
                        lhsT=h_sb[:, s, j * P : (j + 1) * P],
                        rhs=ones[:, 0:ONES],
                        start=True,
                        stop=True,
                    )

            def join_sums(b):
                for c in range(0, BANK, P):
                    j = (b * BANK + c) // P
                    nc.tensor.matmul(
                        out=h_mean[b][:, c : c + P],
                        lhsT=h_sum[:, j : j + 1].to_broadcast([P, P]),
                        rhs=ident_f32[:],
                        start=False,
                        stop=False,
                        is_transpose=True,
                    )

            for s in range(SLICES_BEFORE_JOIN):
                if s in COLUMN_SLICES:
                    sum_slice(s)
                else:
                    for b in range(FEATS // BANK):
                        spread_slice(s, b)
            nc.vector.tensor_reduce(out=h_sum[:], in_=h_part[:, :, :, 0], axis=AXIS.X, op=ALU.add)
            for b in range(FEATS // BANK):
                join_sums(b)
                for s in range(SLICES_BEFORE_JOIN, SLICES):
                    spread_slice(s, b)

            def add_mean(t, b):
                cols = slice(b * BANK, (b + 1) * BANK)
                nc.vector.tensor_tensor(
                    out=e_f32[:, t, cols], in0=e_sb[:, t, cols], in1=h_mean[b][:], op=ALU.add
                )

            def sum_squares(t, cols, total):
                squares = work.tile([P, FEATS], BF16)
                nc.scalar.activation(
                    out=squares[:, cols], in_=e_f32[:, t, cols], func=ACT.Square, accum_out=total
                )

            inv_norms = {}

            def invert_by_gpsimd(tiles):
                count = tiles.stop - tiles.start
                floored_sums = keep.tile([P, count], F32, name="floored_sums%d" % tiles.start)
                powers = keep.tile([P, count], F32, name="powers%d" % tiles.start)
                if tiles.start == 0:
                    nc.gpsimd.tensor_scalar(
                        out=floored_sums[:],
                        in0=first_sums[:, 0:1],
                        scalar1=first_sums[:, 1:2],
                        scalar2=NORM_FLOOR * NORM_FLOOR,
                        op0=ALU.add,
                        op1=ALU.max,
                    )
                else:
                    nc.gpsimd.tensor_scalar(
                        out=floored_sums[:],
                        in0=sumsq[:, tiles],
                        scalar1=NORM_FLOOR * NORM_FLOOR,
                        scalar2=None,
                        op0=ALU.max,
                    )
                nc.gpsimd.tensor_tensor(
                    out=powers[:], in0=floored_sums[:], in1=minus_halves[:, 0:count], op=ALU.pow
                )
                for t in range(tiles.start, tiles.stop):
                    inv_norms[t] = powers[:, t - tiles.start : t - tiles.start + 1]

            def roots(tiles):
                nc.scalar.activation(
                    out=norm[:, tiles], in_=sumsq[:, tiles], func=ACT.Sqrt, bias=SQRT_GUARD
                )

            def invert(tiles):
                nc.vector.tensor_scalar(
                    out=floored[:, tiles],
                    in0=norm[:, tiles],
                    scalar1=NORM_FLOOR,
                    scalar2=None,
                    op0=ALU.max,
                )
                nc.vector.reciprocal(out=inv_norm[:, tiles], in_=floored[:, tiles])
                for t in range(tiles.start, tiles.stop):
                    inv_norms[t] = inv_norm[:, t : t + 1]

            flipped = {}

            def scale_and_flip(t):
                engine = nc.vector if t in SCALED_BY_VECTOR else nc.gpsimd
                e_cur = work.tile([P, FEATS], BF16, bufs=4)
                engine.tensor_scalar(
                    out=e_cur[:].rearrange("p (u w e) -> p u w e", u=PAIRS, e=2),
                    in0=e_f32[:, t, :].rearrange("p (w u e) -> p u w e", u=PAIRS, e=2),
                    scalar1=inv_norms[t],
                    scalar2=0.0,
                    op0=ALU.mult,
                    op1=ALU.add,
                )
                words = e_cur[:].bitcast(F32).rearrange("p (u g q) -> p u g q", u=PAIRS, g=PASSES)
                e_t = bank_tile("e_t%d" % t, RING_START + t % RING, [P, PASSES, PAIRS, P])
                for g in range(PASSES):
                    for u in range(PAIRS):
                        nc.tensor.transpose(e_t[:, g, u, :], words[:, u, g, :], ident_f32[:])
                flipped[t] = e_t
                if t in WARM_AFTER:
                    keep_warm("idle%d" % t, *WARM_AFTER[t])

            def regroup(t):
                copy = nc.vector.tensor_copy if t in REGROUPED_BY_VECTOR else nc.scalar.copy
                copy(
                    out=grouped[t][:].bitcast(F32),
                    in_=flipped[t][:].rearrange("p g u r -> p g r u"),
                )

            def quantise(t):
                nodes = slice(t * P, (t + 1) * P)
                for g in range(PASSES):
                    nc.vector.quantize_mx(
                        out=codes[:, g, nodes].bitcast(FP8X4),
                        scales=scales[:, g, nodes],
                        in_=grouped[t][:, g, :, :].rearrange("p r q -> p (r q)"),
                    )

            for t in range(TILES):
                for b in range(FEATS // BANK):
                    add_mean(t, b)
                    if t == 0:
                        cols = slice(b * BANK, (b + 1) * BANK)
                        sum_squares(t, cols, first_sums[:, b : b + 1])
                if t > 0:
                    sum_squares(t, slice(0, FEATS), sumsq[:, t : t + 1])
                if t == 5:
                    roots(slice(3, 6))
                if t == 7:
                    roots(slice(6, 8))
                if t in INVERTED_BY_GPSIMD:
                    tiles = INVERTED_BY_GPSIMD[t]
                    invert_by_gpsimd(tiles)
                    for u in range(tiles.start, tiles.stop):
                        scale_and_flip(u)
            regroup(0)
            regroup(1)
            invert(slice(3, 6))
            scale_and_flip(3)
            scale_and_flip(4)
            scale_and_flip(5)
            invert(slice(6, 8))
            regroup(2)
            regroup(3)
            scale_and_flip(6)
            scale_and_flip(7)
            quantise(0)
            quantise(1)
            products(0, 0, 2 * P)
            products(1, 0, 2 * P)
            quantise(2)
            quantise(3)
            for t in range(4, TILES):
                regroup(t)
            for t in range(4, TILES):
                quantise(t)

        w_free = [bank_tile("w_free%d" % b, b, [P, BANK]) for b in range(HALVES)]

        def finish(r, b, lo, hi):
            cols = slice(b * BANK + lo, b * BANK + hi)
            nc.vector.scalar_tensor_tensor(
                out=g_sb[:, r, cols],
                in0=w_free[b][:, lo:hi],
                scalar=w_tiles[r],
                in1=g_sb[:, r, cols],
                op0=ALU.add,
                op1=ALU.mult,
            )

        def relu(n):
            i, b = order[n]
            if b == 1 and i < FIRST:
                unused = work.tile([P, BANK], BF16)
                half = unused[:]
            else:
                half = g_sb[:, i, b * BANK : (b + 1) * BANK]
            half_sum = half_sums[:, b, i : i + 1]
            if (i, b) in RELU_BY_VECTOR:
                nc.vector.tensor_scalar(
                    out=half,
                    in0=sums[n][:],
                    scalar1=0.0,
                    scalar2=0.0,
                    op0=ALU.max,
                    op1=ALU.add,
                    accum_out=half_sum,
                )
            else:
                nc.scalar.activation(out=half, in_=sums[n][:], func=ACT.Relu, accum_out=half_sum)

        def double(tiles):
            nc.gpsimd.tensor_scalar(
                out=doubled[:, tiles],
                in0=half_sums[:, 0, tiles],
                scalar1=2.0,
                scalar2=2.0 * ROWSUM_EPS,
                op0=ALU.mult,
                op1=ALU.add,
            )

        w_tiles = {}

        def weigh(tiles):
            count = tiles.stop - tiles.start
            denom = keep.tile([P, count], F32, name="denom%d" % tiles.start)
            w_part = keep.tile([P, count], F32, name="w_part%d" % tiles.start)
            for i in range(tiles.start, tiles.stop):
                w_tiles[i] = w_part[:, i - tiles.start : i - tiles.start + 1]
            if FIRST < tiles.stop <= FIRST + 2:
                nc.gpsimd.tensor_scalar(
                    out=denom[:],
                    in0=half_sums[:, 1, tiles],
                    scalar1=2.0,
                    scalar2=doubled[:, tiles],
                    op0=ALU.mult,
                    op1=ALU.add,
                )
                nc.gpsimd.tensor_tensor(
                    out=w_part[:], in0=denom[:], in1=minus_ones[:, 0:1], op=ALU.pow
                )
            else:
                nc.vector.scalar_tensor_tensor(
                    out=denom[:],
                    in0=half_sums[:, 1, tiles],
                    scalar=2.0,
                    in1=doubled[:, tiles],
                    op0=ALU.mult,
                    op1=ALU.add,
                )
                nc.vector.reciprocal(out=w_part[:], in_=denom[:])

        def spread(tiles):
            for i in range(tiles.start, tiles.stop):
                bank, lo = divmod(i * P, BANK)
                nc.tensor.transpose(
                    w_free[bank][:, lo : lo + P],
                    w_tiles[i].to_broadcast([P, P]),
                    ident_f32[:],
                )

        def store(rows, cols):
            nc.sync.dma_start(out=out_rows[:, rows, cols], in_=g_sb[:, rows, cols])

        def mirror(i):
            m_t = bank_tile("m_t%d" % i, RING_START + i - FIRST, [P, FIRST, P])
            for r in range(FIRST):
                nc.tensor.transpose(m_t[:, r, :], g_sb[:, i, r * P : (r + 1) * P], ident_f32[:])
            mirrors[i] = m_t

        def copy_mirror(i):
            nc.scalar.copy(out=upper[i // 2][:, :, i % 2, :], in_=mirrors[i][:])

        def store_mirrors(i):
            nc.scalar.dma_start(
                out=out_rows[:, 0:FIRST, i * P : (i + 2) * P],
                in_=upper[i // 2][:].rearrange("p r i c -> p r (i c)"),
            )

        upper = {
            j: keep.tile([P, FIRST, 2, P], F32, name="upper%d" % j)
            for j in range(FIRST // 2, TILES // 2)
        }

        mirrors = {}
        units = len(order)
        groups = [slice(0, 2), slice(2, 4)] + [slice(i, i + 1) for i in range(FIRST, TILES)]
        for n in range(AHEAD):
            products(n, 2 * P)
        for n in range(units):
            relu(n)
            if n + AHEAD < units:
                products(n + AHEAD)
            for tiles in groups:
                if (tiles.stop - 1, 0) == order[n]:
                    double(tiles)
                if (tiles.stop - 1, 1) == order[n]:
                    weigh(tiles)
            if n == 5 + 1:
                spread(slice(0, 2))
                for r in (0, 1):
                    finish(r, 0, 0, 2 * P)
                    store(r, slice(0, 2 * P))
            if n == 7 + 1:
                spread(slice(2, 4))
                for r in (0, 1):
                    finish(r, 0, 2 * P, BANK)
                    store(r, slice(2 * P, BANK))
                for r in (2, 3):
                    finish(r, 0, 0, BANK)
                    store(r, slice(0, BANK))
            if order[n][0] >= FIRST and order[n][1] == 1:
                finish(order[n][0], 0, 0, BANK)
                store(order[n][0], slice(0, BANK))
            if n == 13:
                spread(slice(4, 6))
                for r in (4, 5):
                    finish(r, 1, 0, 2 * P)
                    store(r, slice(BANK, BANK + 2 * P))
        mirror(4)
        mirror(5)
        spread(slice(6, 8))
        copy_mirror(4)
        copy_mirror(5)
        store_mirrors(4)
        mirror(6)
        mirror(7)
        copy_mirror(6)
        copy_mirror(7)
        store_mirrors(6)
        for r in (6, 7, 4, 5):
            finish(r, 1, 2 * P if r < 6 else 0, BANK)
            store(r, slice(BANK + (2 * P if r < 6 else 0), NODES))
